import numpy as np
import ml_dtypes


def mxq(x, axis, fmt="e4m3"):
    dtype, down = {"e4m3": (ml_dtypes.float8_e4m3fn, 7), "e5m2": (ml_dtypes.float8_e5m2, 14)}[fmt]
    v = np.moveaxis(np.asarray(x, np.float32).astype(ml_dtypes.bfloat16).astype(np.float64), axis, -1)
    blocks = v.reshape(v.shape[:-1] + (-1, 32))
    amax = np.abs(blocks).max(-1, keepdims=True)
    byte = np.maximum(np.where(amax > 0, np.frexp(amax)[1] - 1 + 127, 0) - down, 1)
    scale = np.exp2(byte - 127.0)
    codes = (blocks / scale).astype(np.float32).astype(dtype).astype(np.float64)
    return np.moveaxis((codes * scale).reshape(v.shape), -1, axis)


WIDE = False


def mx_kscale(k):
    if not WIDE:
        return np.ones(k)
    levels = np.array([10, -10, 5, -5, 0])
    a = np.random.permutation(np.resize(levels, k // 512 * 4)).reshape(k // 512, 4)
    idx = np.arange(k)
    return np.exp2(a[idx // 512, idx % 128 // 32])


BF16 = ml_dtypes.bfloat16


def bf(x):
    return np.asarray(x, np.float32).astype(BF16)


def f64(x):
    return np.asarray(x).astype(np.float64)


E2M1 = np.array([0.0, 0.5, 1.0, 1.5, 2.0, 3.0, 4.0, 6.0, -0.0, -0.5, -1.0, -1.5, -2.0, -3.0, -4.0, -6.0])


def pack_weight(w, fmt):
    k, n = w.shape
    w = f64(bf(w)).reshape(k // 32, 32, n)
    amax = np.abs(w).max(1)
    if fmt == "e4m3":
        byte = np.frexp(amax)[1] - 1 + 127 - 7
    else:
        mant, ex = np.frexp(amax / 6.0)
        byte = np.where(mant > 0.5, ex, ex - 1) + 127
    byte = np.clip(np.where(amax > 0, byte, 1), 1, 254)
    scaled = (w * np.exp2(127.0 - byte)[:, None, :]).reshape(k, n).astype(np.float32)
    by_word = np.ascontiguousarray(scaled.reshape(k // 512, 128, 4, n).transpose(0, 1, 3, 2))
    if fmt == "e4m3":
        words = by_word.astype(ml_dtypes.float8_e4m3fn).view(np.uint8)
    else:
        c = by_word.astype(ml_dtypes.float4_e2m1fn).view(np.uint8) & 0xF
        words = c[..., 0::2] | (c[..., 1::2] << 4)
    return np.ascontiguousarray(words), np.ascontiguousarray(byte.astype(np.uint8).reshape(k // 512, 16, n))


def unpack_weight(words, scales, fmt):
    g, p, n, _ = words.shape
    if fmt == "e4m3":
        vals = np.ascontiguousarray(words).view(ml_dtypes.float8_e4m3fn).astype(np.float64)
    else:
        nib = np.empty((g, p, n, 4), np.uint8)
        nib[..., 0::2] = words & 0xF
        nib[..., 1::2] = words >> 4
        vals = E2M1[nib]
    vals = vals * np.repeat(np.exp2(scales.astype(np.float64) - 127.0), 8, axis=1)[..., None]
    return vals.transpose(0, 1, 3, 2).reshape(g * 512, n)

def pack4(w):
    words, scales = pack_weight(w, "e2m1")
    return words.reshape(words.shape[0], 128, -1), scales


def unpack4(words, scales):
    return unpack_weight(words.reshape(words.shape[0], 128, -1, 2), scales, "e2m1")


B, N, C0, C1, C2, O0, O1, O2 = 2, 16, 512, 4096, 4096, 512, 2048, 512
G = C1 + C2
K = 2 * G


def sigmoid(v):
    return 1.0 / (1.0 + np.exp(-v))


def setup_inputs():
    s = mx_kscale(G)
    ss = np.concatenate([s, s])
    x1 = bf(np.random.random((B, N, C1)) * s[:C1])
    x2 = bf(np.random.random((B, N, N, C2)) * s[C1:])
    W2_words, W2_scales = pack4(np.random.standard_normal((K, O2)) * 2.0 / np.sqrt(K) / ss[:, None])
    b2 = bf(np.random.standard_normal(O2) * 0.3)
    return {"x1": x1,
            "x2": x2,
            "W2_words": W2_words,
            "W2_scales": W2_scales,
            "b2": b2}


def reference(x1, x2, W2_words, W2_scales, b2):
    x1, x2 = f64(x1), f64(x2)
    e1 = np.broadcast_to(x1[:, :, None, :], (B, N, N, C1))
    g = np.concatenate([e1, x2], axis=-1)
    f2 = np.concatenate([g, np.swapaxes(g, 1, 2)], axis=-1)
    return sigmoid((mxq(f2, 3, "e4m3") @ unpack4(W2_words, W2_scales)) + f64(b2))

@@ -1,0 +1,269 @@
+from contextlib import ExitStack
+
+import concourse.mybir as mybir
+from concourse.masks import make_identity
+
+F32 = mybir.dt.float32
+BF16 = mybir.dt.bfloat16
+I32 = mybir.dt.int32
+U32 = mybir.dt.uint32
+U8 = mybir.dt.uint8
+FP8X4 = mybir.dt.float8_e4m3fn_x4
+FP4X4 = mybir.dt.float4_e2m1fn_x4
+ADD = mybir.AluOpType.add
+SIGMOID = mybir.ActivationFunctionType.Sigmoid
+
+P = 128
+SCENES = 2
+OBJECTS = 16
+CHANNELS = 4096
+OUT = 512
+PAIRS_OF_SCENE = OBJECTS * OBJECTS
+PAIRS = SCENES * PAIRS_OF_SCENE
+SINGLES = SCENES * OBJECTS
+K_PASS = 4 * P
+PASSES = CHANNELS // K_PASS
+SECTIONS = 4
+WORDS_OF_PASS = K_PASS // 2
+OUT_TILES = OUT // P
+ROW_TILES = PAIRS // P
+CHUNK = 2
+CHUNKS = PASSES // CHUNK
+X1_PARTS = P // SINGLES
+AS_LIES = 0
+SWAPPED = 1
+X2_SECTION = (1, 3)
+
+FLOPS = 2 * PAIRS * SECTIONS * CHANNELS * OUT
+
+
+def tile_differentiablelogicmachine_pa_k_kernel(tc, x1, x2, W2_words, W2_scales, b2, out):
+    nc = tc.nc
+    with ExitStack() as ctx:
+        keep = ctx.enter_context(tc.tile_pool(name="keep", bufs=1))
+        stage = ctx.enter_context(tc.tile_pool(name="stage", bufs=2))
+        sums = ctx.enter_context(tc.psum_pool(name="sums", bufs=1))
+        work = ctx.enter_context(tc.psum_pool(name="work", bufs=4))
+        ctx.enter_context(tc.manual_schedule())
+
+        x2_sb = keep.tile([P, ROW_TILES, CHANNELS], BF16)
+        x1_sb = keep.tile([P, CHANNELS // X1_PARTS], BF16)
+        w_words = keep.tile([P, SECTIONS * PASSES, 2 * OUT], U8, align_bytes=64)
+        w_scales = keep.tile([P, SECTIONS * PASSES, OUT], U8, align_bytes=64)
+        x2_codes = keep.tile([P, 2, PASSES, PAIRS], U32, align_bytes=64)
+        x2_scales = keep.tile([P, 2, PASSES, PAIRS], U8, align_bytes=64)
+        x1_grouped = keep.tile([P, PASSES, P, 4], BF16, align_bytes=64)
+        x1_codes = keep.tile([P, PASSES, P], U32, align_bytes=64)
+        x1_scales = keep.tile([P, PASSES, P], U8, align_bytes=64)
+        ident = keep.tile([P, P], F32)
+        bias_rows = keep.tile([P, P], BF16)
+        bias_rows_f32 = keep.tile([P, P], F32)
+        bias = keep.tile([P, OUT_TILES], F32)
+        table_warm = keep.tile([P, 1], F32)
+        c_sb = keep.tile([P, OUT_TILES, SINGLES], F32)
+        ac_sum = keep.tile([P, OUT_TILES, PAIRS], F32)
+        y_acc = [sums.tile([P, PAIRS], F32, name="y_acc%d" % m) for m in range(OUT_TILES)]
+
+        x2_words = x2_sb[:].bitcast(F32)
+        x1_words = x1_sb[:].bitcast(F32)
+
+        make_identity(nc, ident[:])
+        nc.gpsimd.memset(x1_grouped[:].bitcast(F32), 0.0)
+        for section in (1, 3, 0, 2):
+            planes = w_scales[:, section * PASSES : (section + 1) * PASSES, :]
+            nc.vector.memset(planes.bitcast(I32), 0)
+        nc.vector.memset(bias_rows[:], 0.0)
+        nc.vector.memset(table_warm[:], 0.0)
+        nc.scalar.activation(out=table_warm[:], in_=table_warm[:], func=SIGMOID)
+
+        x2_rows = x2.rearrange("b i j k -> (b i j) k")
+        words_dram = W2_words.bitcast(I32).rearrange("g p n -> p g n")
+        scales_dram = W2_scales.bitcast(I32).rearrange("g (q r) n -> r q g n", r=4)
+
+        def load_x2(chunk):
+            cols = slice(chunk * CHUNK * K_PASS, (chunk + 1) * CHUNK * K_PASS)
+            for t in range(ROW_TILES):
+                nc.sync.dma_start(out=x2_sb[:, t, cols], in_=x2_rows[t * P : (t + 1) * P, cols])
+
+        def load_words(first_pass, passes):
+            span = slice(first_pass, first_pass + passes)
+            nc.sync.dma_start(out=w_words[:, span, :].bitcast(I32), in_=words_dram[:, span, :])
+
+        def load_scale_rows(section):
+            span = slice(section * PASSES, (section + 1) * PASSES)
+            for r in range(4):
+                for half in range(2):
+                    nc.sync.dma_start(
+                        out=w_scales[32 * half + r : P : 64, span, :].bitcast(I32),
+                        in_=scales_dram[r, half::2, span, :],
+                    )
+
+        def load_x2_weights(chunk):
+            for section in X2_SECTION:
+                load_words(section * PASSES + chunk * CHUNK, CHUNK)
+
+        load_x2(0)
+        nc.sync.dma_start(out=x1_sb[:], in_=x1.rearrange("b n (c k) -> (b n c) k", c=X1_PARTS))
+        nc.sync.dma_start(out=bias_rows[0:OUT_TILES, :], in_=b2.rearrange("(m o) -> m o", m=OUT_TILES))
+        nc.gpsimd.tensor_copy(out=bias_rows_f32[:], in_=bias_rows[:])
+        for section in X2_SECTION:
+            load_scale_rows(section)
+        load_x2_weights(0)
+        for chunk in range(1, CHUNKS):
+            load_x2(chunk)
+            load_x2_weights(chunk)
+        for section in (0, 2):
+            load_scale_rows(section)
+        for section in (0, 2):
+            load_words(section * PASSES, PASSES)
+
+        def transpose_x2(chunk):
+            banks = {}
+            for scene in range(SCENES):
+                for local in range(CHUNK):
+                    first_word = (chunk * CHUNK + local) * WORDS_OF_PASS
+                    xt = work.tile([P, 2, PAIRS_OF_SCENE], F32, tag="work", name="xt")
+                    for u in range(2):
+                        for half in range(2):
+                            nc.tensor.transpose(
+                                xt[:, u, half * P : (half + 1) * P],
+                                x2_words[:, 2 * scene + half, first_word + u : first_word + WORDS_OF_PASS : 2],
+                                ident[:],
+                            )
+                    banks[(scene, local)] = xt
+            return banks
+
+        def regroup_x2(chunk, banks):
+            grouped = stage.tile([P, 2, CHUNK, PAIRS, 4], BF16, align_bytes=64)
+            grouped_words = grouped[:].bitcast(F32)
+            for scene in range(SCENES):
+                copy = nc.scalar.copy if scene == 0 else nc.vector.tensor_copy
+                cols = slice(scene * PAIRS_OF_SCENE, (scene + 1) * PAIRS_OF_SCENE)
+                for local in range(CHUNK):
+                    xt = banks[(scene, local)]
+                    copy(
+                        out=grouped_words[:, AS_LIES, local, cols, :],
+                        in_=xt[:].rearrange("p u r -> p r u"),
+                    )
+                    copy(
+                        out=grouped_words[:, SWAPPED, local, cols, :].rearrange(
+                            "p (i j) u -> p i j u", i=OBJECTS
+                        ),
+                        in_=xt[:].rearrange("p u (j i) -> p i j u", j=OBJECTS),
+                    )
+            for local in range(CHUNK):
+                g = chunk * CHUNK + local
+                for order in (AS_LIES, SWAPPED):
+                    nc.vector.quantize_mx(
+                        out=x2_codes[:, order, g, :].bitcast(FP8X4),
+                        scales=x2_scales[:, order, g, :],
+                        in_=grouped[:, order, local].rearrange("p r t -> p (r t)"),
+                    )
+
+        def weight_of(w_pass, m):
+            return dict(
+                lhsT=w_words[:, w_pass, 2 * m * P : 2 * (m + 1) * P].bitcast(FP4X4),
+                lhsT_scale=w_scales[:, w_pass, m * P : (m + 1) * P],
+            )
+
+        def multiply_x2(chunk):
+            for m in range(OUT_TILES):
+                for local in range(CHUNK):
+                    g = chunk * CHUNK + local
+                    for order in (AS_LIES, SWAPPED):
+                        nc.tensor.matmul_mx(
+                            out=y_acc[m][:],
+                            rhs=x2_codes[:, order, g, :].bitcast(FP8X4),
+                            rhs_scale=x2_scales[:, order, g, :],
+                            start=(g == 0 and order == AS_LIES),
+                            stop=(g == PASSES - 1 and order == SWAPPED),
+                            **weight_of(X2_SECTION[order] * PASSES + g, m),
+                        )
+
+        def transpose_x1_and_bias():
+            x1t = work.tile([P, 2, 2, P], F32, tag="work", name="x1t")
+            for local in range(2):
+                first_word = local * WORDS_OF_PASS
+                for u in range(2):
+                    nc.tensor.transpose(
+                        x1t[:, local, u, :],
+                        x1_words[:, first_word + u : first_word + WORDS_OF_PASS : 2],
+                        ident[:],
+                    )
+            bias_t = work.tile([P, P], F32, tag="work", name="bias_t")
+            nc.tensor.transpose(bias_t[:], bias_rows_f32[:], ident[:])
+            return x1t, bias_t
+
+        def regroup_x1(x1t, bias_t):
+            by_part = x1_grouped[:].bitcast(F32).rearrange("p (c l) n u -> p l c n u", l=2)
+            for local in range(2):
+                nc.scalar.copy(
+                    out=by_part[:, local, :, 0:SINGLES, :],
+                    in_=x1t[:, local].rearrange("p u (r c) -> p c r u", c=X1_PARTS),
+                )
+            nc.scalar.copy(out=bias[:], in_=bias_t[:, 0:OUT_TILES])
+
+        def quantise_x1():
+            nc.vector.quantize_mx(
+                out=x1_codes[:].rearrange("p g n -> p (g n)").bitcast(FP8X4),
+                scales=x1_scales[:].rearrange("p g n -> p (g n)"),
+                in_=x1_grouped[:].rearrange("p g n t -> p (g n t)"),
+            )
+
+        def multiply_x1(section):
+            term = work.tile([P, OUT_TILES, P], F32, tag="work", name="term")
+            for m in range(OUT_TILES):
+                for g in range(PASSES):
+                    nc.tensor.matmul_mx(
+                        out=term[:, m, :],
+                        rhs=x1_codes[:, g, :].bitcast(FP8X4),
+                        rhs_scale=x1_scales[:, g, :],
+                        start=(g == 0),
+                        stop=(g == PASSES - 1),
+                        **weight_of(section * PASSES + g, m),
+                    )
+            return term
+
+        def spread_x1_terms(a_term, c_term):
+            nc.scalar.copy(out=c_sb[:], in_=c_term[:, :, 0:SINGLES])
+            shape = [P, SCENES, OBJECTS, OBJECTS]
+            for m in range(OUT_TILES):
+                a_of_i = a_term[:, m, 0:SINGLES].rearrange("p (b i) -> p b i", b=SCENES)
+                c_of_j = c_sb[:, m, :].rearrange("p (b j) -> p b j", b=SCENES)
+                nc.vector.tensor_tensor(
+                    out=ac_sum[:, m, :].rearrange("p (b i j) -> p b i j", b=SCENES, i=OBJECTS),
+                    in0=a_of_i.unsqueeze(3).to_broadcast(shape),
+                    in1=c_of_j.unsqueeze(2).to_broadcast(shape),
+                    op=ADD,
+                )
+
+        out_by_tile = out.rearrange("b i j o -> (b i j) o").rearrange("(t p) o -> p t o", p=P)
+
+        def join(m):
+            joined = stage.tile([P, PAIRS], F32, bufs=OUT_TILES, name="joined")
+            nc.vector.scalar_tensor_tensor(
+                out=joined[:], in0=y_acc[m][:], scalar=bias[:, m : m + 1], in1=ac_sum[:, m, :], op0=ADD, op1=ADD
+            )
+            return joined
+
+        def finish(m, joined):
+            back = work.tile([P, ROW_TILES, P], F32, tag="work", name="back")
+            for t in range(ROW_TILES):
+                nc.tensor.transpose(back[:, t, :], joined[:, t * P : (t + 1) * P], ident[:])
+            result = stage.tile([P, ROW_TILES, P], F32, bufs=OUT_TILES, name="result")
+            nc.scalar.activation(out=result[:], in_=back[:], func=SIGMOID)
+            nc.sync.dma_start(out=out_by_tile[:, :, m * P : (m + 1) * P], in_=result[:])
+
+        regroup_x2(0, transpose_x2(0))
+        regroup_x1(*transpose_x1_and_bias())
+        for chunk in range(1, CHUNKS):
+            regroup_x2(chunk, transpose_x2(chunk))
+            multiply_x2(chunk - 1)
+        quantise_x1()
+        a_term = multiply_x1(0)
+        c_term = multiply_x1(2)
+        spread_x1_terms(a_term, c_term)
+        multiply_x2(CHUNKS - 1)
+        joined = [join(m) for m in range(OUT_TILES)]
+        for m in range(OUT_TILES):
+            finish(m, joined[m])

@@ -33,6 +33,7 @@ X1_PARTS = P // SINGLES
 AS_LIES = 0
 SWAPPED = 1
 X2_SECTION = (1, 3)
+X1_WITH_CHUNK = 2
 
 FLOPS = 2 * PAIRS * SECTIONS * CHANNELS * OUT
 
@@ -69,51 +70,50 @@ def tile_differentiablelogicmachine_pa_k_kernel(tc, x1, x2, W2_words, W2_scales,
 
         make_identity(nc, ident[:])
         nc.gpsimd.memset(x1_grouped[:].bitcast(F32), 0.0)
-        for section in (1, 3, 0, 2):
+        for section in (1, 2, 3, 0):
             planes = w_scales[:, section * PASSES : (section + 1) * PASSES, :]
             nc.vector.memset(planes.bitcast(I32), 0)
         nc.vector.memset(bias_rows[:], 0.0)
         nc.vector.memset(table_warm[:], 0.0)
         nc.scalar.activation(out=table_warm[:], in_=table_warm[:], func=SIGMOID)
 
-        x2_rows = x2.rearrange("b i j k -> (b i j) k")
+        x2_by_tile = x2.rearrange("b i j k -> (b i j) k").rearrange("(t p) k -> p t k", p=P)
         words_dram = W2_words.bitcast(I32).rearrange("g p n -> p g n")
         scales_dram = W2_scales.bitcast(I32).rearrange("g (q r) n -> r q g n", r=4)
 
         def load_x2(chunk):
             cols = slice(chunk * CHUNK * K_PASS, (chunk + 1) * CHUNK * K_PASS)
-            for t in range(ROW_TILES):
-                nc.sync.dma_start(out=x2_sb[:, t, cols], in_=x2_rows[t * P : (t + 1) * P, cols])
+            for scene in range(SCENES):
+                tiles = slice(2 * scene, 2 * scene + 2)
+                nc.sync.dma_start(out=x2_sb[:, tiles, cols], in_=x2_by_tile[:, tiles, cols])
 
         def load_words(first_pass, passes):
             span = slice(first_pass, first_pass + passes)
             nc.sync.dma_start(out=w_words[:, span, :].bitcast(I32), in_=words_dram[:, span, :])
 
-        def load_scale_rows(section):
-            span = slice(section * PASSES, (section + 1) * PASSES)
+        def load_scale_rows(first_section, sections):
+            span = slice(first_section * PASSES, (first_section + sections) * PASSES)
             for r in range(4):
-                for half in range(2):
-                    nc.sync.dma_start(
-                        out=w_scales[32 * half + r : P : 64, span, :].bitcast(I32),
-                        in_=scales_dram[r, half::2, span, :],
-                    )
+                nc.sync.dma_start(
+                    out=w_scales[r : P : 32, span, :].bitcast(I32), in_=scales_dram[r, :, span, :]
+                )
 
         def load_x2_weights(chunk):
             for section in X2_SECTION:
                 load_words(section * PASSES + chunk * CHUNK, CHUNK)
 
         load_x2(0)
+        load_scale_rows(1, 3)
+        load_x2_weights(0)
+        load_x2(1)
+        load_x2_weights(1)
         nc.sync.dma_start(out=x1_sb[:], in_=x1.rearrange("b n (c k) -> (b n c) k", c=X1_PARTS))
         nc.sync.dma_start(out=bias_rows[0:OUT_TILES, :], in_=b2.rearrange("(m o) -> m o", m=OUT_TILES))
         nc.gpsimd.tensor_copy(out=bias_rows_f32[:], in_=bias_rows[:])
-        for section in X2_SECTION:
-            load_scale_rows(section)
-        load_x2_weights(0)
-        for chunk in range(1, CHUNKS):
+        for chunk in range(2, CHUNKS):
             load_x2(chunk)
             load_x2_weights(chunk)
-        for section in (0, 2):
-            load_scale_rows(section)
+        load_scale_rows(0, 1)
         for section in (0, 2):
             load_words(section * PASSES, PASSES)
 
@@ -137,9 +137,9 @@ def tile_differentiablelogicmachine_pa_k_kernel(tc, x1, x2, W2_words, W2_scales,
             grouped = stage.tile([P, 2, CHUNK, PAIRS, 4], BF16, align_bytes=64)
             grouped_words = grouped[:].bitcast(F32)
             for scene in range(SCENES):
-                copy = nc.scalar.copy if scene == 0 else nc.vector.tensor_copy
                 cols = slice(scene * PAIRS_OF_SCENE, (scene + 1) * PAIRS_OF_SCENE)
                 for local in range(CHUNK):
+                    copy = nc.vector.tensor_copy if (scene, local) == (1, 0) else nc.scalar.copy
                     xt = banks[(scene, local)]
                     copy(
                         out=grouped_words[:, AS_LIES, local, cols, :],
@@ -255,11 +255,12 @@ def tile_differentiablelogicmachine_pa_k_kernel(tc, x1, x2, W2_words, W2_scales,
             nc.sync.dma_start(out=out_by_tile[:, :, m * P : (m + 1) * P], in_=result[:])
 
         regroup_x2(0, transpose_x2(0))
-        regroup_x1(*transpose_x1_and_bias())
         for chunk in range(1, CHUNKS):
             regroup_x2(chunk, transpose_x2(chunk))
+            if chunk == X1_WITH_CHUNK:
+                regroup_x1(*transpose_x1_and_bias())
+                quantise_x1()
             multiply_x2(chunk - 1)
-        quantise_x1()
         a_term = multiply_x1(0)
         c_term = multiply_x1(2)
         spread_x1_terms(a_term, c_term)

@@ -47,7 +47,7 @@ def tile_differentiablelogicmachine_pa_k_kernel(tc, x1, x2, W2_words, W2_scales,
         work = ctx.enter_context(tc.psum_pool(name="work", bufs=4))
         ctx.enter_context(tc.manual_schedule())
 
-        x2_sb = keep.tile([P, ROW_TILES, CHANNELS], BF16)
+        x2_sb = keep.tile([P, CHUNKS, ROW_TILES, CHUNK * K_PASS], BF16)
         x1_sb = keep.tile([P, CHANNELS // X1_PARTS], BF16)
         w_words = keep.tile([P, SECTIONS * PASSES, 2 * OUT], U8, align_bytes=64)
         w_scales = keep.tile([P, SECTIONS * PASSES, OUT], U8, align_bytes=64)
@@ -85,7 +85,7 @@ def tile_differentiablelogicmachine_pa_k_kernel(tc, x1, x2, W2_words, W2_scales,
             cols = slice(chunk * CHUNK * K_PASS, (chunk + 1) * CHUNK * K_PASS)
             for scene in range(SCENES):
                 tiles = slice(2 * scene, 2 * scene + 2)
-                nc.sync.dma_start(out=x2_sb[:, tiles, cols], in_=x2_by_tile[:, tiles, cols])
+                nc.sync.dma_start(out=x2_sb[:, chunk, tiles, :], in_=x2_by_tile[:, tiles, cols])
 
         def load_words(first_pass, passes):
             span = slice(first_pass, first_pass + passes)
@@ -121,13 +121,13 @@ def tile_differentiablelogicmachine_pa_k_kernel(tc, x1, x2, W2_words, W2_scales,
             banks = {}
             for scene in range(SCENES):
                 for local in range(CHUNK):
-                    first_word = (chunk * CHUNK + local) * WORDS_OF_PASS
+                    first_word = local * WORDS_OF_PASS
                     xt = work.tile([P, 2, PAIRS_OF_SCENE], F32, tag="work", name="xt")
                     for u in range(2):
                         for half in range(2):
                             nc.tensor.transpose(
                                 xt[:, u, half * P : (half + 1) * P],
-                                x2_words[:, 2 * scene + half, first_word + u : first_word + WORDS_OF_PASS : 2],
+                                x2_words[:, chunk, 2 * scene + half, first_word + u : first_word + WORDS_OF_PASS : 2],
                                 ident[:],
                             )
                     banks[(scene, local)] = xt

@@ -33,6 +33,8 @@ X1_PARTS = P // SINGLES
 AS_LIES = 0
 SWAPPED = 1
 X2_SECTION = (1, 3)
+X1_SECTION = (0, 2)
+SCALE_RUN = 4
 X1_WITH_CHUNK = 2
 
 FLOPS = 2 * PAIRS * SECTIONS * CHANNELS * OUT
@@ -70,7 +72,7 @@ def tile_differentiablelogicmachine_pa_k_kernel(tc, x1, x2, W2_words, W2_scales,
 
         make_identity(nc, ident[:])
         nc.gpsimd.memset(x1_grouped[:].bitcast(F32), 0.0)
-        for section in (1, 2, 3, 0):
+        for section in X2_SECTION + X1_SECTION:
             planes = w_scales[:, section * PASSES : (section + 1) * PASSES, :]
             nc.vector.memset(planes.bitcast(I32), 0)
         nc.vector.memset(bias_rows[:], 0.0)
@@ -91,8 +93,8 @@ def tile_differentiablelogicmachine_pa_k_kernel(tc, x1, x2, W2_words, W2_scales,
             span = slice(first_pass, first_pass + passes)
             nc.sync.dma_start(out=w_words[:, span, :].bitcast(I32), in_=words_dram[:, span, :])
 
-        def load_scale_rows(first_section, sections):
-            span = slice(first_section * PASSES, (first_section + sections) * PASSES)
+        def load_scale_rows(first_pass):
+            span = slice(first_pass, first_pass + SCALE_RUN)
             for r in range(4):
                 nc.sync.dma_start(
                     out=w_scales[r : P : 32, span, :].bitcast(I32), in_=scales_dram[r, :, span, :]
@@ -103,19 +105,26 @@ def tile_differentiablelogicmachine_pa_k_kernel(tc, x1, x2, W2_words, W2_scales,
                 load_words(section * PASSES + chunk * CHUNK, CHUNK)
 
         load_x2(0)
-        load_scale_rows(1, 3)
+        for section in X2_SECTION:
+            load_scale_rows(section * PASSES)
         load_x2_weights(0)
         load_x2(1)
         load_x2_weights(1)
         nc.sync.dma_start(out=x1_sb[:], in_=x1.rearrange("b n (c k) -> (b n c) k", c=X1_PARTS))
         nc.sync.dma_start(out=bias_rows[0:OUT_TILES, :], in_=b2.rearrange("(m o) -> m o", m=OUT_TILES))
         nc.gpsimd.tensor_copy(out=bias_rows_f32[:], in_=bias_rows[:])
-        for chunk in range(2, CHUNKS):
-            load_x2(chunk)
-            load_x2_weights(chunk)
-        load_scale_rows(0, 1)
-        for section in (0, 2):
-            load_words(section * PASSES, PASSES)
+        load_x2(2)
+        for section in X2_SECTION:
+            load_scale_rows(section * PASSES + SCALE_RUN)
+        load_x2(3)
+        load_x2_weights(2)
+        for section in X1_SECTION:
+            for first_pass in range(section * PASSES, (section + 1) * PASSES, SCALE_RUN):
+                load_scale_rows(first_pass)
+        for section in X1_SECTION:
+            for first_pass in range(section * PASSES, (section + 1) * PASSES, SCALE_RUN):
+                load_words(first_pass, SCALE_RUN)
+        load_x2_weights(3)
 
         def transpose_x2(chunk):
             banks = {}

@@ -27,7 +27,7 @@ SECTIONS = 4
 WORDS_OF_PASS = K_PASS // 2
 OUT_TILES = OUT // P
 ROW_TILES = PAIRS // P
-CHUNK = 2
+CHUNK = 1
 CHUNKS = PASSES // CHUNK
 X1_PARTS = P // SINGLES
 AS_LIES = 0
@@ -35,7 +35,8 @@ SWAPPED = 1
 X2_SECTION = (1, 3)
 X1_SECTION = (0, 2)
 SCALE_RUN = 4
-X1_WITH_CHUNK = 2
+WORDS_RUN = 2
+X1_WITH_CHUNK = CHUNKS // 2
 
 FLOPS = 2 * PAIRS * SECTIONS * CHANNELS * OUT
 
@@ -83,11 +84,10 @@ def tile_differentiablelogicmachine_pa_k_kernel(tc, x1, x2, W2_words, W2_scales,
         words_dram = W2_words.bitcast(I32).rearrange("g p n -> p g n")
         scales_dram = W2_scales.bitcast(I32).rearrange("g (q r) n -> r q g n", r=4)
 
-        def load_x2(chunk):
-            cols = slice(chunk * CHUNK * K_PASS, (chunk + 1) * CHUNK * K_PASS)
-            for scene in range(SCENES):
-                tiles = slice(2 * scene, 2 * scene + 2)
-                nc.sync.dma_start(out=x2_sb[:, chunk, tiles, :], in_=x2_by_tile[:, tiles, cols])
+        def load_x2(first_pass):
+            for chunk in range(first_pass // CHUNK, (first_pass + WORDS_RUN) // CHUNK):
+                cols = slice(chunk * CHUNK * K_PASS, (chunk + 1) * CHUNK * K_PASS)
+                nc.sync.dma_start(out=x2_sb[:, chunk, :, :], in_=x2_by_tile[:, :, cols])
 
         def load_words(first_pass, passes):
             span = slice(first_pass, first_pass + passes)
@@ -100,31 +100,33 @@ def tile_differentiablelogicmachine_pa_k_kernel(tc, x1, x2, W2_words, W2_scales,
                     out=w_scales[r : P : 32, span, :].bitcast(I32), in_=scales_dram[r, :, span, :]
                 )
 
-        def load_x2_weights(chunk):
+        def load_x2_scale_rows(first_pass):
             for section in X2_SECTION:
-                load_words(section * PASSES + chunk * CHUNK, CHUNK)
+                load_scale_rows(section * PASSES + first_pass)
+
+        def load_x2_words(first_pass):
+            for section in X2_SECTION:
+                load_words(section * PASSES + first_pass, WORDS_RUN)
 
         load_x2(0)
-        for section in X2_SECTION:
-            load_scale_rows(section * PASSES)
-        load_x2_weights(0)
-        load_x2(1)
-        load_x2_weights(1)
+        load_x2_scale_rows(0)
+        load_x2_words(0)
+        load_x2(2)
+        load_x2_words(2)
         nc.sync.dma_start(out=x1_sb[:], in_=x1.rearrange("b n (c k) -> (b n c) k", c=X1_PARTS))
         nc.sync.dma_start(out=bias_rows[0:OUT_TILES, :], in_=b2.rearrange("(m o) -> m o", m=OUT_TILES))
         nc.gpsimd.tensor_copy(out=bias_rows_f32[:], in_=bias_rows[:])
-        load_x2(2)
-        for section in X2_SECTION:
-            load_scale_rows(section * PASSES + SCALE_RUN)
-        load_x2(3)
-        load_x2_weights(2)
+        load_x2(4)
+        load_x2_scale_rows(4)
+        load_x2_words(4)
+        load_x2(6)
         for section in X1_SECTION:
             for first_pass in range(section * PASSES, (section + 1) * PASSES, SCALE_RUN):
                 load_scale_rows(first_pass)
         for section in X1_SECTION:
             for first_pass in range(section * PASSES, (section + 1) * PASSES, SCALE_RUN):
                 load_words(first_pass, SCALE_RUN)
-        load_x2_weights(3)
+        load_x2_words(6)
 
         def transpose_x2(chunk):
             banks = {}
@@ -143,7 +145,7 @@ def tile_differentiablelogicmachine_pa_k_kernel(tc, x1, x2, W2_words, W2_scales,
             return banks
 
         def regroup_x2(chunk, banks):
-            grouped = stage.tile([P, 2, CHUNK, PAIRS, 4], BF16, align_bytes=64)
+            grouped = stage.tile([P, 2, CHUNK, PAIRS, 4], BF16, bufs=3, align_bytes=64)
             grouped_words = grouped[:].bitcast(F32)
             for scene in range(SCENES):
                 cols = slice(scene * PAIRS_OF_SCENE, (scene + 1) * PAIRS_OF_SCENE)
@@ -264,15 +266,17 @@ def tile_differentiablelogicmachine_pa_k_kernel(tc, x1, x2, W2_words, W2_scales,
             nc.sync.dma_start(out=out_by_tile[:, :, m * P : (m + 1) * P], in_=result[:])
 
         regroup_x2(0, transpose_x2(0))
-        for chunk in range(1, CHUNKS):
+        for chunk in range(1, CHUNKS - 1):
             regroup_x2(chunk, transpose_x2(chunk))
             if chunk == X1_WITH_CHUNK:
                 regroup_x1(*transpose_x1_and_bias())
                 quantise_x1()
             multiply_x2(chunk - 1)
-        a_term = multiply_x1(0)
-        c_term = multiply_x1(2)
+        regroup_x2(CHUNKS - 1, transpose_x2(CHUNKS - 1))
+        a_term = multiply_x1(X1_SECTION[0])
+        c_term = multiply_x1(X1_SECTION[1])
         spread_x1_terms(a_term, c_term)
+        multiply_x2(CHUNKS - 2)
         multiply_x2(CHUNKS - 1)
         joined = [join(m) for m in range(OUT_TILES)]
         for m in range(OUT_TILES):

@@ -11,7 +11,10 @@ U8 = mybir.dt.uint8
 FP8X4 = mybir.dt.float8_e4m3fn_x4
 FP4X4 = mybir.dt.float4_e2m1fn_x4
 ADD = mybir.AluOpType.add
+SUBTRACT = mybir.AluOpType.subtract
+MULT = mybir.AluOpType.mult
 SIGMOID = mybir.ActivationFunctionType.Sigmoid
+AXES_XY = mybir.AxisListType.XY
 
 P = 128
 SCENES = 2
@@ -25,18 +28,16 @@ K_PASS = 4 * P
 PASSES = CHANNELS // K_PASS
 SECTIONS = 4
 WORDS_OF_PASS = K_PASS // 2
-OUT_TILES = OUT // P
 ROW_TILES = PAIRS // P
-CHUNK = 1
-CHUNKS = PASSES // CHUNK
 X1_PARTS = P // SINGLES
+HALF = P // 2
 AS_LIES = 0
 SWAPPED = 1
 X2_SECTION = (1, 3)
 X1_SECTION = (0, 2)
 SCALE_RUN = 4
 WORDS_RUN = 2
-X1_WITH_CHUNK = CHUNKS // 2
+X1_WITH_PASS = PASSES // 2
 
 FLOPS = 2 * PAIRS * SECTIONS * CHANNELS * OUT
 
@@ -45,49 +46,70 @@ def tile_differentiablelogicmachine_pa_k_kernel(tc, x1, x2, W2_words, W2_scales,
     nc = tc.nc
     with ExitStack() as ctx:
         keep = ctx.enter_context(tc.tile_pool(name="keep", bufs=1))
-        stage = ctx.enter_context(tc.tile_pool(name="stage", bufs=2))
+        stage = ctx.enter_context(tc.tile_pool(name="stage", bufs=3))
         sums = ctx.enter_context(tc.psum_pool(name="sums", bufs=1))
         work = ctx.enter_context(tc.psum_pool(name="work", bufs=4))
         ctx.enter_context(tc.manual_schedule())
 
-        x2_sb = keep.tile([P, CHUNKS, ROW_TILES, CHUNK * K_PASS], BF16)
+        x2_sb = keep.tile([P, PASSES, ROW_TILES, K_PASS], BF16)
         x1_sb = keep.tile([P, CHANNELS // X1_PARTS], BF16)
         w_words = keep.tile([P, SECTIONS * PASSES, 2 * OUT], U8, align_bytes=64)
-        w_scales = keep.tile([P, SECTIONS * PASSES, OUT], U8, align_bytes=64)
+        w_scales = [
+            keep.tile([P, SCALE_RUN, OUT], U8, align_bytes=64, name="w_scales%d" % run)
+            for run in range(SECTIONS * PASSES // SCALE_RUN)
+        ]
         x2_codes = keep.tile([P, 2, PASSES, PAIRS], U32, align_bytes=64)
         x2_scales = keep.tile([P, 2, PASSES, PAIRS], U8, align_bytes=64)
-        x1_grouped = keep.tile([P, PASSES, P, 4], BF16, align_bytes=64)
-        x1_codes = keep.tile([P, PASSES, P], U32, align_bytes=64)
-        x1_scales = keep.tile([P, PASSES, P], U8, align_bytes=64)
+        x1_grouped = keep.tile([P, PASSES, 2, HALF, 4], BF16, align_bytes=64)
+        x1_codes = keep.tile([P, PASSES * P + HALF], U32, align_bytes=64)
+        x1_scales = keep.tile([P, PASSES * P + HALF], U8, align_bytes=64)
         ident = keep.tile([P, P], F32)
-        bias_rows = keep.tile([P, P], BF16)
-        bias_rows_f32 = keep.tile([P, P], F32)
-        bias = keep.tile([P, OUT_TILES], F32)
+        a_hot = keep.tile([P, SINGLES], BF16)
+        c_hot = keep.tile([P, SINGLES], BF16)
+        hot = keep.tile([P, PAIRS], BF16)
+        low_rows = keep.tile([P, 1], F32)
+        bias_row = keep.tile([P, OUT], BF16)
+        half_tile = keep.tile([P, P], BF16)
+        bias_half = keep.tile([P, OUT], F32)
         table_warm = keep.tile([P, 1], F32)
-        c_sb = keep.tile([P, OUT_TILES, SINGLES], F32)
-        ac_sum = keep.tile([P, OUT_TILES, PAIRS], F32)
-        y_acc = [sums.tile([P, PAIRS], F32, name="y_acc%d" % m) for m in range(OUT_TILES)]
+        terms = keep.tile([P, OUT], F32)
+        terms_high = keep.tile([P, OUT], BF16)
+        terms_split = keep.tile([P, OUT], BF16)
+        y_acc = [sums.tile([P, OUT], F32, name="y_acc%d" % t) for t in range(ROW_TILES)]
 
         x2_words = x2_sb[:].bitcast(F32)
         x1_words = x1_sb[:].bitcast(F32)
 
         make_identity(nc, ident[:])
-        nc.gpsimd.memset(x1_grouped[:].bitcast(F32), 0.0)
         for section in X2_SECTION + X1_SECTION:
-            planes = w_scales[:, section * PASSES : (section + 1) * PASSES, :]
-            nc.vector.memset(planes.bitcast(I32), 0)
-        nc.vector.memset(bias_rows[:], 0.0)
+            for run in range(section * PASSES // SCALE_RUN, (section + 1) * PASSES // SCALE_RUN):
+                nc.vector.memset(w_scales[run][:].bitcast(I32), 0)
+        nc.vector.memset(bias_row[:], 0.0)
+        nc.vector.memset(half_tile[:], 0.5)
         nc.vector.memset(table_warm[:], 0.0)
         nc.scalar.activation(out=table_warm[:], in_=table_warm[:], func=SIGMOID)
+        nc.gpsimd.memset(x1_grouped[:].bitcast(F32)[:, :, 0, :, :], 0.0)
+        nc.gpsimd.memset(x1_codes[:, PASSES * P :], 0)
+        nc.gpsimd.memset(x1_scales[:, PASSES * P :], 0)
+        pair_shape = [P, SCENES, OBJECTS, OBJECTS]
+        nc.gpsimd.tensor_tensor(out=a_hot[:], in0=ident[:, 0:32], in1=ident[:, 32:64], op=ADD)
+        nc.gpsimd.tensor_tensor(out=c_hot[:], in0=ident[:, 64:96], in1=ident[:, 96:128], op=ADD)
+        nc.gpsimd.tensor_tensor(
+            out=hot[:].rearrange("p (b i j) -> p b i j", b=SCENES, i=OBJECTS),
+            in0=a_hot[:].rearrange("p (b i) -> p b i", b=SCENES).unsqueeze(3).to_broadcast(pair_shape),
+            in1=c_hot[:].rearrange("p (b j) -> p b j", b=SCENES).unsqueeze(2).to_broadcast(pair_shape),
+            op=ADD,
+        )
 
         x2_by_tile = x2.rearrange("b i j k -> (b i j) k").rearrange("(t p) k -> p t k", p=P)
         words_dram = W2_words.bitcast(I32).rearrange("g p n -> p g n")
         scales_dram = W2_scales.bitcast(I32).rearrange("g (q r) n -> r q g n", r=4)
 
         def load_x2(first_pass):
-            for chunk in range(first_pass // CHUNK, (first_pass + WORDS_RUN) // CHUNK):
-                cols = slice(chunk * CHUNK * K_PASS, (chunk + 1) * CHUNK * K_PASS)
-                nc.sync.dma_start(out=x2_sb[:, chunk, :, :], in_=x2_by_tile[:, :, cols])
+            for g in range(first_pass, first_pass + WORDS_RUN):
+                nc.sync.dma_start(
+                    out=x2_sb[:, g, :, :], in_=x2_by_tile[:, :, g * K_PASS : (g + 1) * K_PASS]
+                )
 
         def load_words(first_pass, passes):
             span = slice(first_pass, first_pass + passes)
@@ -97,7 +119,8 @@ def tile_differentiablelogicmachine_pa_k_kernel(tc, x1, x2, W2_words, W2_scales,
             span = slice(first_pass, first_pass + SCALE_RUN)
             for r in range(4):
                 nc.sync.dma_start(
-                    out=w_scales[r : P : 32, span, :].bitcast(I32), in_=scales_dram[r, :, span, :]
+                    out=w_scales[first_pass // SCALE_RUN][r : P : 32, :, :].bitcast(I32),
+                    in_=scales_dram[r, :, span, :],
                 )
 
         def load_x2_scale_rows(first_pass):
@@ -114,8 +137,7 @@ def tile_differentiablelogicmachine_pa_k_kernel(tc, x1, x2, W2_words, W2_scales,
         load_x2(2)
         load_x2_words(2)
         nc.sync.dma_start(out=x1_sb[:], in_=x1.rearrange("b n (c k) -> (b n c) k", c=X1_PARTS))
-        nc.sync.dma_start(out=bias_rows[0:OUT_TILES, :], in_=b2.rearrange("(m o) -> m o", m=OUT_TILES))
-        nc.gpsimd.tensor_copy(out=bias_rows_f32[:], in_=bias_rows[:])
+        nc.sync.dma_start(out=bias_row[0:1, :], in_=b2.rearrange("(m o) -> m o", m=1))
         load_x2(4)
         load_x2_scale_rows(4)
         load_x2_words(4)
@@ -128,70 +150,58 @@ def tile_differentiablelogicmachine_pa_k_kernel(tc, x1, x2, W2_words, W2_scales,
                 load_words(first_pass, SCALE_RUN)
         load_x2_words(6)
 
-        def transpose_x2(chunk):
-            banks = {}
+        def transpose_x2(g):
+            banks = []
             for scene in range(SCENES):
-                for local in range(CHUNK):
-                    first_word = local * WORDS_OF_PASS
-                    xt = work.tile([P, 2, PAIRS_OF_SCENE], F32, tag="work", name="xt")
-                    for u in range(2):
-                        for half in range(2):
-                            nc.tensor.transpose(
-                                xt[:, u, half * P : (half + 1) * P],
-                                x2_words[:, chunk, 2 * scene + half, first_word + u : first_word + WORDS_OF_PASS : 2],
-                                ident[:],
-                            )
-                    banks[(scene, local)] = xt
+                xt = work.tile([P, 2, PAIRS_OF_SCENE], F32, tag="work", name="xt")
+                for u in range(2):
+                    for half in range(2):
+                        nc.tensor.transpose(
+                            xt[:, u, half * P : (half + 1) * P],
+                            x2_words[:, g, 2 * scene + half, u:WORDS_OF_PASS:2],
+                            ident[:],
+                        )
+                banks.append(xt)
             return banks
 
-        def regroup_x2(chunk, banks):
-            grouped = stage.tile([P, 2, CHUNK, PAIRS, 4], BF16, bufs=3, align_bytes=64)
+        def regroup_x2(g, banks):
+            grouped = stage.tile([P, PAIRS, 4], BF16, align_bytes=64)
             grouped_words = grouped[:].bitcast(F32)
             for scene in range(SCENES):
                 cols = slice(scene * PAIRS_OF_SCENE, (scene + 1) * PAIRS_OF_SCENE)
-                for local in range(CHUNK):
-                    copy = nc.vector.tensor_copy if (scene, local) == (1, 0) else nc.scalar.copy
-                    xt = banks[(scene, local)]
-                    copy(
-                        out=grouped_words[:, AS_LIES, local, cols, :],
-                        in_=xt[:].rearrange("p u r -> p r u"),
-                    )
-                    copy(
-                        out=grouped_words[:, SWAPPED, local, cols, :].rearrange(
-                            "p (i j) u -> p i j u", i=OBJECTS
-                        ),
-                        in_=xt[:].rearrange("p u (j i) -> p i j u", j=OBJECTS),
-                    )
-            for local in range(CHUNK):
-                g = chunk * CHUNK + local
-                for order in (AS_LIES, SWAPPED):
-                    nc.vector.quantize_mx(
-                        out=x2_codes[:, order, g, :].bitcast(FP8X4),
-                        scales=x2_scales[:, order, g, :],
-                        in_=grouped[:, order, local].rearrange("p r t -> p (r t)"),
-                    )
+                copy = nc.vector.tensor_copy if (g == 0 and scene == 1) else nc.scalar.copy
+                copy(out=grouped_words[:, cols, :], in_=banks[scene][:].rearrange("p u r -> p r u"))
+            nc.vector.quantize_mx(
+                out=x2_codes[:, AS_LIES, g, :].bitcast(FP8X4),
+                scales=x2_scales[:, AS_LIES, g, :],
+                in_=grouped[:].rearrange("p r t -> p (r t)"),
+            )
+            for plane in (x2_codes[:].bitcast(I32), x2_scales[:]):
+                nc.vector.tensor_copy(
+                    out=plane[:, SWAPPED, g, :].rearrange("p (b q r j) -> p b q j r", b=SCENES, q=4, r=4),
+                    in_=plane[:, AS_LIES, g, :].rearrange("p (b j q r) -> p b q j r", b=SCENES, q=4, r=4),
+                )
 
-        def weight_of(w_pass, m):
+        def weight(section, g):
+            w_pass = section * PASSES + g
             return dict(
-                lhsT=w_words[:, w_pass, 2 * m * P : 2 * (m + 1) * P].bitcast(FP4X4),
-                lhsT_scale=w_scales[:, w_pass, m * P : (m + 1) * P],
+                rhs=w_words[:, w_pass, :].bitcast(FP4X4),
+                rhs_scale=w_scales[w_pass // SCALE_RUN][:, w_pass % SCALE_RUN, :],
             )
 
-        def multiply_x2(chunk):
-            for m in range(OUT_TILES):
-                for local in range(CHUNK):
-                    g = chunk * CHUNK + local
-                    for order in (AS_LIES, SWAPPED):
-                        nc.tensor.matmul_mx(
-                            out=y_acc[m][:],
-                            rhs=x2_codes[:, order, g, :].bitcast(FP8X4),
-                            rhs_scale=x2_scales[:, order, g, :],
-                            start=(g == 0 and order == AS_LIES),
-                            stop=(g == PASSES - 1 and order == SWAPPED),
-                            **weight_of(X2_SECTION[order] * PASSES + g, m),
-                        )
+        def multiply_x2(t, g):
+            cols = slice(t * P, (t + 1) * P)
+            for order in (AS_LIES, SWAPPED):
+                nc.tensor.matmul_mx(
+                    out=y_acc[t][:],
+                    lhsT=x2_codes[:, order, g, cols].bitcast(FP8X4),
+                    lhsT_scale=x2_scales[:, order, g, cols],
+                    start=(g == 0 and order == AS_LIES),
+                    stop=(g == PASSES - 1 and order == SWAPPED),
+                    **weight(X2_SECTION[order], g),
+                )
 
-        def transpose_x1_and_bias():
+        def transpose_x1_and_spread_bias():
             x1t = work.tile([P, 2, 2, P], F32, tag="work", name="x1t")
             for local in range(2):
                 first_word = local * WORDS_OF_PASS
@@ -201,83 +211,86 @@ def tile_differentiablelogicmachine_pa_k_kernel(tc, x1, x2, W2_words, W2_scales,
                         x1_words[:, first_word + u : first_word + WORDS_OF_PASS : 2],
                         ident[:],
                     )
-            bias_t = work.tile([P, P], F32, tag="work", name="bias_t")
-            nc.tensor.transpose(bias_t[:], bias_rows_f32[:], ident[:])
-            return x1t, bias_t
+            bias_all = work.tile([P, OUT], F32, tag="work", name="bias_all")
+            nc.tensor.matmul(bias_all[:], lhsT=half_tile[:], rhs=bias_row[:], start=True, stop=True)
+            return x1t, bias_all
 
-        def regroup_x1(x1t, bias_t):
-            by_part = x1_grouped[:].bitcast(F32).rearrange("p (c l) n u -> p l c n u", l=2)
+        def regroup_x1(x1t, bias_all):
+            by_part = x1_grouped[:].bitcast(F32).rearrange("p (c l) h (k n) u -> p l h k c n u", l=2, k=2)
             for local in range(2):
-                nc.scalar.copy(
-                    out=by_part[:, local, :, 0:SINGLES, :],
-                    in_=x1t[:, local].rearrange("p u (r c) -> p c r u", c=X1_PARTS),
-                )
-            nc.scalar.copy(out=bias[:], in_=bias_t[:, 0:OUT_TILES])
-
-        def quantise_x1():
-            nc.vector.quantize_mx(
-                out=x1_codes[:].rearrange("p g n -> p (g n)").bitcast(FP8X4),
-                scales=x1_scales[:].rearrange("p g n -> p (g n)"),
-                in_=x1_grouped[:].rearrange("p g n t -> p (g n t)"),
-            )
-
-        def multiply_x1(section):
-            term = work.tile([P, OUT_TILES, P], F32, tag="work", name="term")
-            for m in range(OUT_TILES):
-                for g in range(PASSES):
-                    nc.tensor.matmul_mx(
-                        out=term[:, m, :],
-                        rhs=x1_codes[:, g, :].bitcast(FP8X4),
-                        rhs_scale=x1_scales[:, g, :],
-                        start=(g == 0),
-                        stop=(g == PASSES - 1),
-                        **weight_of(section * PASSES + g, m),
+                for copy_of_x1 in range(2):
+                    nc.scalar.copy(
+                        out=by_part[:, local, 1, copy_of_x1],
+                        in_=x1t[:, local].rearrange("p u (r c) -> p c r u", c=X1_PARTS),
                     )
-            return term
-
-        def spread_x1_terms(a_term, c_term):
-            nc.scalar.copy(out=c_sb[:], in_=c_term[:, :, 0:SINGLES])
-            shape = [P, SCENES, OBJECTS, OBJECTS]
-            for m in range(OUT_TILES):
-                a_of_i = a_term[:, m, 0:SINGLES].rearrange("p (b i) -> p b i", b=SCENES)
-                c_of_j = c_sb[:, m, :].rearrange("p (b j) -> p b j", b=SCENES)
-                nc.vector.tensor_tensor(
-                    out=ac_sum[:, m, :].rearrange("p (b i j) -> p b i j", b=SCENES, i=OBJECTS),
-                    in0=a_of_i.unsqueeze(3).to_broadcast(shape),
-                    in1=c_of_j.unsqueeze(2).to_broadcast(shape),
-                    op=ADD,
-                )
-
-        out_by_tile = out.rearrange("b i j o -> (b i j) o").rearrange("(t p) o -> p t o", p=P)
-
-        def join(m):
-            joined = stage.tile([P, PAIRS], F32, bufs=OUT_TILES, name="joined")
-            nc.vector.scalar_tensor_tensor(
-                out=joined[:], in0=y_acc[m][:], scalar=bias[:, m : m + 1], in1=ac_sum[:, m, :], op0=ADD, op1=ADD
+            nc.scalar.copy(out=bias_half[:], in_=bias_all[:])
+            nc.vector.quantize_mx(
+                out=x1_codes[:, 0 : PASSES * P].bitcast(FP8X4),
+                scales=x1_scales[:, 0 : PASSES * P],
+                in_=x1_grouped[:].rearrange("p g h n t -> p (g h n t)"),
             )
-            return joined
+            nc.vector.tensor_reduce(
+                out=low_rows[:],
+                in_=ident[:].rearrange("p (h q r) -> p h q r", h=2, q=2)[:, :, 1, :],
+                axis=AXES_XY,
+                op=ADD,
+            )
 
-        def finish(m, joined):
-            back = work.tile([P, ROW_TILES, P], F32, tag="work", name="back")
+        def multiply_x1():
+            ac = work.tile([P, OUT], F32, tag="work", name="ac")
+            for section, first in ((X1_SECTION[0], HALF), (X1_SECTION[1], 0)):
+                for g in range(PASSES):
+                    cols = slice(g * P + first, (g + 1) * P + first)
+                    nc.tensor.matmul_mx(
+                        out=ac[:],
+                        lhsT=x1_codes[:, cols].bitcast(FP8X4),
+                        lhsT_scale=x1_scales[:, cols],
+                        start=(section == X1_SECTION[0] and g == 0),
+                        stop=(section == X1_SECTION[1] and g == PASSES - 1),
+                        **weight(section, g),
+                    )
+            return ac
+
+        def split_terms(ac):
+            nc.vector.tensor_tensor(out=terms[:], in0=ac[:], in1=bias_half[:], op=ADD)
+            nc.vector.tensor_copy(out=terms_high[:], in_=terms[:])
+            nc.vector.scalar_tensor_tensor(
+                out=terms_split[:], in0=terms_high[:], scalar=low_rows[:], in1=terms[:], op0=MULT, op1=SUBTRACT
+            )
+
+        def spread_terms():
+            spread = []
             for t in range(ROW_TILES):
-                nc.tensor.transpose(back[:, t, :], joined[:, t * P : (t + 1) * P], ident[:])
-            result = stage.tile([P, ROW_TILES, P], F32, bufs=OUT_TILES, name="result")
-            nc.scalar.activation(out=result[:], in_=back[:], func=SIGMOID)
-            nc.sync.dma_start(out=out_by_tile[:, :, m * P : (m + 1) * P], in_=result[:])
+                bank = work.tile([P, OUT], F32, tag="work", name="spread")
+                nc.tensor.matmul(bank[:], lhsT=hot[:, t * P : (t + 1) * P], rhs=terms_split[:], start=True, stop=True)
+                minus_terms = stage.tile([P, OUT], F32, bufs=ROW_TILES, name="minus_terms")
+                nc.scalar.copy(out=minus_terms[:], in_=bank[:])
+                spread.append(minus_terms)
+            return spread
+
+        out_by_tile = out.rearrange("b i j o -> (b i j) o").rearrange("(t p) o -> t p o", p=P)
+
+        def finish(t, minus_terms):
+            joined = stage.tile([P, OUT], F32, bufs=ROW_TILES, name="joined")
+            nc.vector.tensor_tensor(out=joined[:], in0=y_acc[t][:], in1=minus_terms[:], op=SUBTRACT)
+            result = stage.tile([P, OUT], F32, bufs=ROW_TILES, name="result")
+            nc.scalar.activation(out=result[:], in_=joined[:], func=SIGMOID)
+            nc.sync.dma_start(out=out_by_tile[t], in_=result[:])
 
         regroup_x2(0, transpose_x2(0))
-        for chunk in range(1, CHUNKS - 1):
-            regroup_x2(chunk, transpose_x2(chunk))
-            if chunk == X1_WITH_CHUNK:
-                regroup_x1(*transpose_x1_and_bias())
-                quantise_x1()
-            multiply_x2(chunk - 1)
-        regroup_x2(CHUNKS - 1, transpose_x2(CHUNKS - 1))
-        a_term = multiply_x1(X1_SECTION[0])
-        c_term = multiply_x1(X1_SECTION[1])
-        spread_x1_terms(a_term, c_term)
-        multiply_x2(CHUNKS - 2)
-        multiply_x2(CHUNKS - 1)
-        joined = [join(m) for m in range(OUT_TILES)]
-        for m in range(OUT_TILES):
-            finish(m, joined[m])
+        for g in range(1, PASSES - 2):
+            regroup_x2(g, transpose_x2(g))
+            if g == X1_WITH_PASS:
+                regroup_x1(*transpose_x1_and_spread_bias())
+            for t in range(ROW_TILES):
+                multiply_x2(t, g - 1)
+        for g in (PASSES - 2, PASSES - 1):
+            regroup_x2(g, transpose_x2(g))
+        split_terms(multiply_x1())
+        for t in range(ROW_TILES):
+            multiply_x2(t, PASSES - 3)
+        spread = spread_terms()
+        for t in range(ROW_TILES):
+            for g in (PASSES - 2, PASSES - 1):
+                multiply_x2(t, g)
+            finish(t, spread[t])

@@ -35,9 +35,9 @@ AS_LIES = 0
 SWAPPED = 1
 X2_SECTION = (1, 3)
 X1_SECTION = (0, 2)
-SCALE_RUN = 4
-WORDS_RUN = 2
-X1_WITH_PASS = PASSES // 2
+RUN = 2
+SINGLE = 2 * RUN
+X1_WITH_RUN = 2
 
 FLOPS = 2 * PAIRS * SECTIONS * CHANNELS * OUT
 
@@ -51,13 +51,14 @@ def tile_differentiablelogicmachine_pa_k_kernel(tc, x1, x2, W2_words, W2_scales,
         work = ctx.enter_context(tc.psum_pool(name="work", bufs=4))
         ctx.enter_context(tc.manual_schedule())
 
-        x2_sb = keep.tile([P, PASSES, ROW_TILES, K_PASS], BF16)
+        x2_first = keep.tile([P, SINGLE, ROW_TILES, K_PASS], BF16)
+        x2_later = {
+            run: keep.tile([P, ROW_TILES, RUN * K_PASS], BF16, name="x2_later%d" % run)
+            for run in range(SINGLE // RUN, PASSES // RUN)
+        }
         x1_sb = keep.tile([P, CHANNELS // X1_PARTS], BF16)
         w_words = keep.tile([P, SECTIONS * PASSES, 2 * OUT], U8, align_bytes=64)
-        w_scales = [
-            keep.tile([P, SCALE_RUN, OUT], U8, align_bytes=64, name="w_scales%d" % run)
-            for run in range(SECTIONS * PASSES // SCALE_RUN)
-        ]
+        w_scales = [keep.tile([P, PASSES, OUT], U8, align_bytes=64, name="w_scales%d" % s) for s in range(SECTIONS)]
         x2_codes = keep.tile([P, 2, PASSES, PAIRS], U32, align_bytes=64)
         x2_scales = keep.tile([P, 2, PASSES, PAIRS], U8, align_bytes=64)
         x1_grouped = keep.tile([P, PASSES, 2, HALF, 4], BF16, align_bytes=64)
@@ -77,17 +78,18 @@ def tile_differentiablelogicmachine_pa_k_kernel(tc, x1, x2, W2_words, W2_scales,
         terms_split = keep.tile([P, OUT], BF16)
         y_acc = [sums.tile([P, OUT], F32, name="y_acc%d" % t) for t in range(ROW_TILES)]
 
-        x2_words = x2_sb[:].bitcast(F32)
+        first_words = x2_first[:].bitcast(F32)
         x1_words = x1_sb[:].bitcast(F32)
 
+        nc.gpsimd.memset(w_scales[X2_SECTION[1]][:].bitcast(I32), 0)
         make_identity(nc, ident[:])
-        for section in X2_SECTION + X1_SECTION:
-            for run in range(section * PASSES // SCALE_RUN, (section + 1) * PASSES // SCALE_RUN):
-                nc.vector.memset(w_scales[run][:].bitcast(I32), 0)
-        nc.vector.memset(bias_row[:], 0.0)
-        nc.vector.memset(half_tile[:], 0.5)
+        nc.vector.memset(w_scales[X2_SECTION[0]][:].bitcast(I32), 0)
         nc.vector.memset(table_warm[:], 0.0)
         nc.scalar.activation(out=table_warm[:], in_=table_warm[:], func=SIGMOID)
+        nc.vector.memset(bias_row[:], 0.0)
+        nc.vector.memset(half_tile[:], 0.5)
+        for section in X1_SECTION:
+            nc.gpsimd.memset(w_scales[section][:].bitcast(I32), 0)
         nc.gpsimd.memset(x1_grouped[:].bitcast(F32)[:, :, 0, :, :], 0.0)
         nc.gpsimd.memset(x1_codes[:, PASSES * P :], 0)
         nc.gpsimd.memset(x1_scales[:, PASSES * P :], 0)
@@ -105,52 +107,63 @@ def tile_differentiablelogicmachine_pa_k_kernel(tc, x1, x2, W2_words, W2_scales,
         words_dram = W2_words.bitcast(I32).rearrange("g p n -> p g n")
         scales_dram = W2_scales.bitcast(I32).rearrange("g (q r) n -> r q g n", r=4)
 
-        def load_x2(first_pass):
-            for g in range(first_pass, first_pass + WORDS_RUN):
-                nc.sync.dma_start(
-                    out=x2_sb[:, g, :, :], in_=x2_by_tile[:, :, g * K_PASS : (g + 1) * K_PASS]
-                )
+        def load_x2_later(run):
+            cols = slice(run * RUN * K_PASS, (run + 1) * RUN * K_PASS)
+            nc.sync.dma_start(out=x2_later[run][:], in_=x2_by_tile[:, :, cols])
 
         def load_words(first_pass, passes):
             span = slice(first_pass, first_pass + passes)
             nc.sync.dma_start(out=w_words[:, span, :].bitcast(I32), in_=words_dram[:, span, :])
 
-        def load_scale_rows(first_pass):
-            span = slice(first_pass, first_pass + SCALE_RUN)
+        def load_scale_rows(section):
+            span = slice(section * PASSES, (section + 1) * PASSES)
             for r in range(4):
+                nc.sync.dma_start(out=w_scales[section][r:P:32, :, :].bitcast(I32), in_=scales_dram[r, :, span, :])
+
+        def load_x2_words(run):
+            for section in X2_SECTION:
+                load_words(section * PASSES + run * RUN, RUN)
+
+        def load_x2_first(g, halves):
+            for half in range(halves):
+                tiles = slice(half * ROW_TILES // halves, (half + 1) * ROW_TILES // halves)
                 nc.sync.dma_start(
-                    out=w_scales[first_pass // SCALE_RUN][r : P : 32, :, :].bitcast(I32),
-                    in_=scales_dram[r, :, span, :],
+                    out=x2_first[:, g, tiles, :], in_=x2_by_tile[:, tiles, g * K_PASS : (g + 1) * K_PASS]
                 )
 
-        def load_x2_scale_rows(first_pass):
-            for section in X2_SECTION:
-                load_scale_rows(section * PASSES + first_pass)
-
-        def load_x2_words(first_pass):
-            for section in X2_SECTION:
-                load_words(section * PASSES + first_pass, WORDS_RUN)
-
-        load_x2(0)
-        load_x2_scale_rows(0)
+        load_x2_first(0, 2)
+        load_x2_first(1, 1)
+        load_scale_rows(X2_SECTION[0])
         load_x2_words(0)
-        load_x2(2)
-        load_x2_words(2)
+        load_scale_rows(X2_SECTION[1])
+        for g in range(RUN, SINGLE):
+            load_x2_first(g, 1)
+        load_x2_words(1)
         nc.sync.dma_start(out=x1_sb[:], in_=x1.rearrange("b n (c k) -> (b n c) k", c=X1_PARTS))
         nc.sync.dma_start(out=bias_row[0:1, :], in_=b2.rearrange("(m o) -> m o", m=1))
-        load_x2(4)
-        load_x2_scale_rows(4)
-        load_x2_words(4)
-        load_x2(6)
+        load_x2_later(2)
+        load_x2_words(2)
+        load_x2_later(3)
         for section in X1_SECTION:
-            for first_pass in range(section * PASSES, (section + 1) * PASSES, SCALE_RUN):
-                load_scale_rows(first_pass)
+            load_scale_rows(section)
         for section in X1_SECTION:
-            for first_pass in range(section * PASSES, (section + 1) * PASSES, SCALE_RUN):
-                load_words(first_pass, SCALE_RUN)
-        load_x2_words(6)
+            load_words(section * PASSES, PASSES)
+        load_x2_words(3)
 
-        def transpose_x2(g):
+        def first_planes(g):
+            return lambda t, u: first_words[:, g, t, u:WORDS_OF_PASS:2]
+
+        def sort_x2(g):
+            if g < SINGLE:
+                words = first_words[:, g, :, :]
+            else:
+                cols = slice((g % RUN) * WORDS_OF_PASS, (g % RUN + 1) * WORDS_OF_PASS)
+                words = x2_later[g // RUN][:].bitcast(F32)[:, :, cols]
+            ordered = stage.tile([P, ROW_TILES, 2, P], F32, bufs=2 * RUN, name="ordered")
+            nc.vector.tensor_copy(out=ordered[:], in_=words.rearrange("p t (w u) -> p t u w", u=2))
+            return lambda t, u: ordered[:, t, u, :]
+
+        def transpose_x2(planes):
             banks = []
             for scene in range(SCENES):
                 xt = work.tile([P, 2, PAIRS_OF_SCENE], F32, tag="work", name="xt")
@@ -158,7 +171,7 @@ def tile_differentiablelogicmachine_pa_k_kernel(tc, x1, x2, W2_words, W2_scales,
                     for half in range(2):
                         nc.tensor.transpose(
                             xt[:, u, half * P : (half + 1) * P],
-                            x2_words[:, g, 2 * scene + half, u:WORDS_OF_PASS:2],
+                            planes(2 * scene + half, u),
                             ident[:],
                         )
                 banks.append(xt)
@@ -169,29 +182,41 @@ def tile_differentiablelogicmachine_pa_k_kernel(tc, x1, x2, W2_words, W2_scales,
             grouped_words = grouped[:].bitcast(F32)
             for scene in range(SCENES):
                 cols = slice(scene * PAIRS_OF_SCENE, (scene + 1) * PAIRS_OF_SCENE)
-                copy = nc.vector.tensor_copy if (g == 0 and scene == 1) else nc.scalar.copy
+                copy = nc.vector.tensor_copy if (g <= RUN and scene == 1) else nc.scalar.copy
                 copy(out=grouped_words[:, cols, :], in_=banks[scene][:].rearrange("p u r -> p r u"))
+            return grouped
+
+        def quantise_x2(g, grouped, first_scene, scenes):
+            cols = slice(first_scene * PAIRS_OF_SCENE, (first_scene + scenes) * PAIRS_OF_SCENE)
             nc.vector.quantize_mx(
-                out=x2_codes[:, AS_LIES, g, :].bitcast(FP8X4),
-                scales=x2_scales[:, AS_LIES, g, :],
-                in_=grouped[:].rearrange("p r t -> p (r t)"),
+                out=x2_codes[:, AS_LIES, g, cols].bitcast(FP8X4),
+                scales=x2_scales[:, AS_LIES, g, cols],
+                in_=grouped[:, cols, :].rearrange("p r t -> p (r t)"),
             )
+
+        def swap_x2(g):
             for plane in (x2_codes[:].bitcast(I32), x2_scales[:]):
                 nc.vector.tensor_copy(
                     out=plane[:, SWAPPED, g, :].rearrange("p (b q r j) -> p b q j r", b=SCENES, q=4, r=4),
                     in_=plane[:, AS_LIES, g, :].rearrange("p (b j q r) -> p b q j r", b=SCENES, q=4, r=4),
                 )
 
+        def prepare_x2(g, banks):
+            grouped = regroup_x2(g, banks)
+            if g == 0:
+                for scene in range(SCENES):
+                    quantise_x2(g, grouped, scene, 1)
+            else:
+                quantise_x2(g, grouped, 0, SCENES)
+            swap_x2(g)
+
         def weight(section, g):
             w_pass = section * PASSES + g
-            return dict(
-                rhs=w_words[:, w_pass, :].bitcast(FP4X4),
-                rhs_scale=w_scales[w_pass // SCALE_RUN][:, w_pass % SCALE_RUN, :],
-            )
+            return dict(rhs=w_words[:, w_pass, :].bitcast(FP4X4), rhs_scale=w_scales[section][:, g, :])
 
-        def multiply_x2(t, g):
+        def multiply_x2(t, g, orders=(AS_LIES, SWAPPED)):
             cols = slice(t * P, (t + 1) * P)
-            for order in (AS_LIES, SWAPPED):
+            for order in orders:
                 nc.tensor.matmul_mx(
                     out=y_acc[t][:],
                     lhsT=x2_codes[:, order, g, cols].bitcast(FP8X4),
@@ -277,18 +302,35 @@ def tile_differentiablelogicmachine_pa_k_kernel(tc, x1, x2, W2_words, W2_scales,
             nc.scalar.activation(out=result[:], in_=joined[:], func=SIGMOID)
             nc.sync.dma_start(out=out_by_tile[t], in_=result[:])
 
-        regroup_x2(0, transpose_x2(0))
-        for g in range(1, PASSES - 2):
-            regroup_x2(g, transpose_x2(g))
-            if g == X1_WITH_PASS:
-                regroup_x1(*transpose_x1_and_spread_bias())
+        def multiply_order(g, order):
             for t in range(ROW_TILES):
-                multiply_x2(t, g - 1)
-        for g in (PASSES - 2, PASSES - 1):
-            regroup_x2(g, transpose_x2(g))
+                multiply_x2(t, g, (order,))
+
+        def multiply_all(g):
+            multiply_order(g, AS_LIES)
+            multiply_order(g, SWAPPED)
+
+        banks = [transpose_x2(first_planes(g)) for g in range(RUN)]
+        for g in range(RUN):
+            prepare_x2(g, banks[g])
+        multiply_all(0)
+        for run in range(1, PASSES // RUN):
+            planes = [sort_x2(g) for g in range(run * RUN, (run + 1) * RUN)]
+            if run == 1:
+                multiply_order(run * RUN - 1, AS_LIES)
+            banks = [transpose_x2(p) for p in planes]
+            for g in range(RUN):
+                prepare_x2(run * RUN + g, banks[g])
+            if run == X1_WITH_RUN:
+                regroup_x1(*transpose_x1_and_spread_bias())
+            if run == 1:
+                multiply_order(run * RUN - 1, SWAPPED)
+                multiply_all(run * RUN)
+            elif run < PASSES // RUN - 1:
+                multiply_all(run * RUN - 1)
+                multiply_all(run * RUN)
         split_terms(multiply_x1())
-        for t in range(ROW_TILES):
-            multiply_x2(t, PASSES - 3)
+        multiply_all(PASSES - RUN - 1)
         spread = spread_terms()
         for t in range(ROW_TILES):
             for g in (PASSES - 2, PASSES - 1):

@@ -37,6 +37,9 @@ X2_SECTION = (1, 3)
 X1_SECTION = (0, 2)
 RUN = 2
 SINGLE = 2 * RUN
+SCALE_RUNS = ((0, 2), (2, 4), (4, 8))
+PIECES = 4
+LAST_TILE = ROW_TILES - 1
 X1_WITH_RUN = 2
 
 FLOPS = 2 * PAIRS * SECTIONS * CHANNELS * OUT
@@ -58,7 +61,13 @@ def tile_differentiablelogicmachine_pa_k_kernel(tc, x1, x2, W2_words, W2_scales,
         }
         x1_sb = keep.tile([P, CHANNELS // X1_PARTS], BF16)
         w_words = keep.tile([P, SECTIONS * PASSES, 2 * OUT], U8, align_bytes=64)
-        w_scales = [keep.tile([P, PASSES, OUT], U8, align_bytes=64, name="w_scales%d" % s) for s in range(SECTIONS)]
+        scale_runs = {s: SCALE_RUNS if s in X2_SECTION else ((0, PASSES),) for s in range(SECTIONS)}
+        w_scales = {}
+        for section, runs in scale_runs.items():
+            for first, end in runs:
+                w_scales[section, first] = keep.tile(
+                    [P, end - first, OUT], U8, align_bytes=64, name="w_scales%d_%d" % (section, first)
+                )
         x2_codes = keep.tile([P, 2, PASSES, PAIRS], U32, align_bytes=64)
         x2_scales = keep.tile([P, 2, PASSES, PAIRS], U8, align_bytes=64)
         x1_grouped = keep.tile([P, PASSES, 2, HALF, 4], BF16, align_bytes=64)
@@ -73,6 +82,7 @@ def tile_differentiablelogicmachine_pa_k_kernel(tc, x1, x2, W2_words, W2_scales,
         half_tile = keep.tile([P, P], BF16)
         bias_half = keep.tile([P, OUT], F32)
         table_warm = keep.tile([P, 1], F32)
+        sigmoid_warm = keep.tile([P, 1], F32)
         terms = keep.tile([P, OUT], F32)
         terms_high = keep.tile([P, OUT], BF16)
         terms_split = keep.tile([P, OUT], BF16)
@@ -81,18 +91,22 @@ def tile_differentiablelogicmachine_pa_k_kernel(tc, x1, x2, W2_words, W2_scales,
         first_words = x2_first[:].bitcast(F32)
         x1_words = x1_sb[:].bitcast(F32)
 
-        nc.gpsimd.memset(w_scales[X2_SECTION[1]][:].bitcast(I32), 0)
         make_identity(nc, ident[:])
-        nc.vector.memset(w_scales[X2_SECTION[0]][:].bitcast(I32), 0)
         nc.vector.memset(table_warm[:], 0.0)
-        nc.scalar.activation(out=table_warm[:], in_=table_warm[:], func=SIGMOID)
-        nc.vector.memset(bias_row[:], 0.0)
-        nc.vector.memset(half_tile[:], 0.5)
+        for first, end in SCALE_RUNS:
+            for section in X2_SECTION:
+                nc.vector.memset(w_scales[section, first][:].bitcast(I32), 0)
+        nc.scalar.copy(
+            out=x1_grouped[:].bitcast(F32)[:, :, 0, :, :].rearrange("p g n u -> p g (n u)"),
+            in_=table_warm[:].unsqueeze(2).to_broadcast([P, PASSES, 2 * HALF]),
+        )
+        nc.scalar.activation(out=sigmoid_warm[:], in_=table_warm[:], func=SIGMOID)
         for section in X1_SECTION:
-            nc.gpsimd.memset(w_scales[section][:].bitcast(I32), 0)
-        nc.gpsimd.memset(x1_grouped[:].bitcast(F32)[:, :, 0, :, :], 0.0)
+            nc.gpsimd.memset(w_scales[section, 0][:].bitcast(I32), 0)
         nc.gpsimd.memset(x1_codes[:, PASSES * P :], 0)
         nc.gpsimd.memset(x1_scales[:, PASSES * P :], 0)
+        nc.vector.memset(bias_row[:], 0.0)
+        nc.vector.memset(half_tile[:], 0.5)
         pair_shape = [P, SCENES, OBJECTS, OBJECTS]
         nc.gpsimd.tensor_tensor(out=a_hot[:], in0=ident[:, 0:32], in1=ident[:, 32:64], op=ADD)
         nc.gpsimd.tensor_tensor(out=c_hot[:], in0=ident[:, 64:96], in1=ident[:, 96:128], op=ADD)
@@ -115,10 +129,13 @@ def tile_differentiablelogicmachine_pa_k_kernel(tc, x1, x2, W2_words, W2_scales,
             span = slice(first_pass, first_pass + passes)
             nc.sync.dma_start(out=w_words[:, span, :].bitcast(I32), in_=words_dram[:, span, :])
 
-        def load_scale_rows(section):
-            span = slice(section * PASSES, (section + 1) * PASSES)
+        def load_scale_rows(section, run):
+            first, end = scale_runs[section][run]
+            span = slice(section * PASSES + first, section * PASSES + end)
             for r in range(4):
-                nc.sync.dma_start(out=w_scales[section][r:P:32, :, :].bitcast(I32), in_=scales_dram[r, :, span, :])
+                nc.sync.dma_start(
+                    out=w_scales[section, first][r:P:32, :, :].bitcast(I32), in_=scales_dram[r, :, span, :]
+                )
 
         def load_x2_words(run):
             for section in X2_SECTION:
@@ -133,21 +150,25 @@ def tile_differentiablelogicmachine_pa_k_kernel(tc, x1, x2, W2_words, W2_scales,
 
         load_x2_first(0, 2)
         load_x2_first(1, 1)
-        load_scale_rows(X2_SECTION[0])
+        load_scale_rows(1, 0)
         load_x2_words(0)
-        load_scale_rows(X2_SECTION[1])
-        for g in range(RUN, SINGLE):
-            load_x2_first(g, 1)
+        load_scale_rows(3, 0)
+        load_x2_first(2, 1)
+        load_scale_rows(1, 1)
+        load_x2_first(3, 1)
+        load_scale_rows(3, 1)
         load_x2_words(1)
         nc.sync.dma_start(out=x1_sb[:], in_=x1.rearrange("b n (c k) -> (b n c) k", c=X1_PARTS))
         nc.sync.dma_start(out=bias_row[0:1, :], in_=b2.rearrange("(m o) -> m o", m=1))
         load_x2_later(2)
+        load_scale_rows(1, 2)
         load_x2_words(2)
+        load_scale_rows(3, 2)
         load_x2_later(3)
-        for section in X1_SECTION:
-            load_scale_rows(section)
-        for section in X1_SECTION:
-            load_words(section * PASSES, PASSES)
+        load_scale_rows(0, 0)
+        load_words(0, PASSES)
+        load_scale_rows(2, 0)
+        load_words(2 * PASSES, PASSES)
         load_x2_words(3)
 
         def first_planes(g):
@@ -210,19 +231,24 @@ def tile_differentiablelogicmachine_pa_k_kernel(tc, x1, x2, W2_words, W2_scales,
                 quantise_x2(g, grouped, 0, SCENES)
             swap_x2(g)
 
-        def weight(section, g):
+        def weight(section, g, first=0, width=OUT):
             w_pass = section * PASSES + g
-            return dict(rhs=w_words[:, w_pass, :].bitcast(FP4X4), rhs_scale=w_scales[section][:, g, :])
+            run_start = max(start for start, end in scale_runs[section] if start <= g)
+            return dict(
+                rhs=w_words[:, w_pass, 2 * first : 2 * (first + width)].bitcast(FP4X4),
+                rhs_scale=w_scales[section, run_start][:, g - run_start, first : first + width],
+            )
 
         def multiply_x2(t, g, orders=(AS_LIES, SWAPPED)):
             cols = slice(t * P, (t + 1) * P)
+            last_pass = PASSES - RUN - 1 if t == LAST_TILE else PASSES - 1
             for order in orders:
                 nc.tensor.matmul_mx(
                     out=y_acc[t][:],
                     lhsT=x2_codes[:, order, g, cols].bitcast(FP8X4),
                     lhsT_scale=x2_scales[:, order, g, cols],
                     start=(g == 0 and order == AS_LIES),
-                    stop=(g == PASSES - 1 and order == SWAPPED),
+                    stop=(g == last_pass and order == SWAPPED),
                     **weight(X2_SECTION[order], g),
                 )
 
@@ -289,7 +315,8 @@ def tile_differentiablelogicmachine_pa_k_kernel(tc, x1, x2, W2_words, W2_scales,
                 bank = work.tile([P, OUT], F32, tag="work", name="spread")
                 nc.tensor.matmul(bank[:], lhsT=hot[:, t * P : (t + 1) * P], rhs=terms_split[:], start=True, stop=True)
                 minus_terms = stage.tile([P, OUT], F32, bufs=ROW_TILES, name="minus_terms")
-                nc.scalar.copy(out=minus_terms[:], in_=bank[:])
+                copy = nc.scalar.copy if t % 2 == 0 else nc.vector.tensor_copy
+                copy(out=minus_terms[:], in_=bank[:])
                 spread.append(minus_terms)
             return spread
 
@@ -301,6 +328,36 @@ def tile_differentiablelogicmachine_pa_k_kernel(tc, x1, x2, W2_words, W2_scales,
             result = stage.tile([P, OUT], F32, bufs=ROW_TILES, name="result")
             nc.scalar.activation(out=result[:], in_=joined[:], func=SIGMOID)
             nc.sync.dma_start(out=out_by_tile[t], in_=result[:])
+
+        def multiply_piece(piece):
+            width = OUT // PIECES
+            bank = work.tile([P, width], F32, tag="work", name="piece")
+            cols = slice(LAST_TILE * P, PAIRS)
+            for g in range(PASSES - RUN, PASSES):
+                for order in (AS_LIES, SWAPPED):
+                    nc.tensor.matmul_mx(
+                        out=bank[:],
+                        lhsT=x2_codes[:, order, g, cols].bitcast(FP8X4),
+                        lhsT_scale=x2_scales[:, order, g, cols],
+                        start=(g == PASSES - RUN and order == AS_LIES),
+                        stop=(g == PASSES - 1 and order == SWAPPED),
+                        **weight(X2_SECTION[order], g, piece * width, width),
+                    )
+            return bank
+
+        def join_last(minus_terms):
+            joined = stage.tile([P, OUT], F32, bufs=ROW_TILES, name="joined")
+            nc.vector.tensor_tensor(out=joined[:], in0=y_acc[LAST_TILE][:], in1=minus_terms[:], op=SUBTRACT)
+            return joined
+
+        def finish_piece(piece, bank, joined):
+            width = OUT // PIECES
+            cols = slice(piece * width, (piece + 1) * width)
+            whole = stage.tile([P, width], F32, bufs=PIECES, name="whole")
+            nc.vector.tensor_tensor(out=whole[:], in0=bank[:], in1=joined[:, cols], op=ADD)
+            result = stage.tile([P, width], F32, bufs=PIECES, name="piece_result")
+            nc.scalar.activation(out=result[:], in_=whole[:], func=SIGMOID)
+            nc.sync.dma_start(out=out_by_tile[LAST_TILE][:, cols], in_=result[:])
 
         def multiply_order(g, order):
             for t in range(ROW_TILES):
@@ -332,7 +389,11 @@ def tile_differentiablelogicmachine_pa_k_kernel(tc, x1, x2, W2_words, W2_scales,
         split_terms(multiply_x1())
         multiply_all(PASSES - RUN - 1)
         spread = spread_terms()
-        for t in range(ROW_TILES):
-            for g in (PASSES - 2, PASSES - 1):
+        for t in range(LAST_TILE):
+            for g in range(PASSES - RUN, PASSES):
                 multiply_x2(t, g)
             finish(t, spread[t])
+            if t == 0:
+                joined = join_last(spread[LAST_TILE])
+        for piece in range(PIECES):
+            finish_piece(piece, multiply_piece(piece), joined)

@@ -171,18 +171,12 @@ def tile_differentiablelogicmachine_pa_k_kernel(tc, x1, x2, W2_words, W2_scales,
         load_words(2 * PASSES, PASSES)
         load_x2_words(3)
 
-        def first_planes(g):
-            return lambda t, u: first_words[:, g, t, u:WORDS_OF_PASS:2]
-
-        def sort_x2(g):
+        def word_planes(g):
             if g < SINGLE:
-                words = first_words[:, g, :, :]
-            else:
-                cols = slice((g % RUN) * WORDS_OF_PASS, (g % RUN + 1) * WORDS_OF_PASS)
-                words = x2_later[g // RUN][:].bitcast(F32)[:, :, cols]
-            ordered = stage.tile([P, ROW_TILES, 2, P], F32, bufs=2 * RUN, name="ordered")
-            nc.vector.tensor_copy(out=ordered[:], in_=words.rearrange("p t (w u) -> p t u w", u=2))
-            return lambda t, u: ordered[:, t, u, :]
+                return lambda t, u: first_words[:, g, t, u:WORDS_OF_PASS:2]
+            words = x2_later[g // RUN][:].bitcast(F32)
+            first = (g % RUN) * WORDS_OF_PASS
+            return lambda t, u: words[:, t, first + u : first + WORDS_OF_PASS : 2]
 
         def transpose_x2(planes):
             banks = []
@@ -367,15 +361,14 @@ def tile_differentiablelogicmachine_pa_k_kernel(tc, x1, x2, W2_words, W2_scales,
             multiply_order(g, AS_LIES)
             multiply_order(g, SWAPPED)
 
-        banks = [transpose_x2(first_planes(g)) for g in range(RUN)]
+        banks = [transpose_x2(word_planes(g)) for g in range(RUN)]
         for g in range(RUN):
             prepare_x2(g, banks[g])
         multiply_all(0)
         for run in range(1, PASSES // RUN):
-            planes = [sort_x2(g) for g in range(run * RUN, (run + 1) * RUN)]
             if run == 1:
                 multiply_order(run * RUN - 1, AS_LIES)
-            banks = [transpose_x2(p) for p in planes]
+            banks = [transpose_x2(word_planes(run * RUN + g)) for g in range(RUN)]
             for g in range(RUN):
                 prepare_x2(run * RUN + g, banks[g])
             if run == X1_WITH_RUN:

@@ -38,9 +38,12 @@ X1_SECTION = (0, 2)
 RUN = 2
 SINGLE = 2 * RUN
 SCALE_RUNS = ((0, 2), (2, 4), (4, 8))
+WARM_BEFORE = 7
+WARM_BETWEEN = 2
+WARM_AFTER = 4
 PIECES = 4
 LAST_TILE = ROW_TILES - 1
-X1_WITH_RUN = 2
+X1_WITH_PASS = 4
 
 FLOPS = 2 * PAIRS * SECTIONS * CHANNELS * OUT
 
@@ -80,6 +83,7 @@ def tile_differentiablelogicmachine_pa_k_kernel(tc, x1, x2, W2_words, W2_scales,
         low_rows = keep.tile([P, 1], F32)
         bias_row = keep.tile([P, OUT], BF16)
         half_tile = keep.tile([P, P], BF16)
+        zero_row = keep.tile([P, OUT], BF16)
         bias_half = keep.tile([P, OUT], F32)
         table_warm = keep.tile([P, 1], F32)
         sigmoid_warm = keep.tile([P, 1], F32)
@@ -92,21 +96,23 @@ def tile_differentiablelogicmachine_pa_k_kernel(tc, x1, x2, W2_words, W2_scales,
         x1_words = x1_sb[:].bitcast(F32)
 
         make_identity(nc, ident[:])
+        nc.vector.memset(half_tile[:], 0.5)
+        nc.vector.memset(zero_row[:].bitcast(I32), 0)
         nc.vector.memset(table_warm[:], 0.0)
-        for first, end in SCALE_RUNS:
-            for section in X2_SECTION:
-                nc.vector.memset(w_scales[section, first][:].bitcast(I32), 0)
+        for section, runs in scale_runs.items():
+            if section in X2_SECTION:
+                for first, end in runs:
+                    nc.vector.memset(w_scales[section, first][:].bitcast(I32), 0)
+        nc.vector.memset(bias_row[:].bitcast(I32), 0)
+        for section in X1_SECTION:
+            nc.vector.memset(w_scales[section, 0][:].bitcast(I32), 0)
+        nc.vector.memset(x1_codes[:, PASSES * P :], 0)
+        nc.vector.memset(x1_scales[:, PASSES * P :].bitcast(I32), 0)
         nc.scalar.copy(
             out=x1_grouped[:].bitcast(F32)[:, :, 0, :, :].rearrange("p g n u -> p g (n u)"),
             in_=table_warm[:].unsqueeze(2).to_broadcast([P, PASSES, 2 * HALF]),
         )
         nc.scalar.activation(out=sigmoid_warm[:], in_=table_warm[:], func=SIGMOID)
-        for section in X1_SECTION:
-            nc.gpsimd.memset(w_scales[section, 0][:].bitcast(I32), 0)
-        nc.gpsimd.memset(x1_codes[:, PASSES * P :], 0)
-        nc.gpsimd.memset(x1_scales[:, PASSES * P :], 0)
-        nc.vector.memset(bias_row[:], 0.0)
-        nc.vector.memset(half_tile[:], 0.5)
         pair_shape = [P, SCENES, OBJECTS, OBJECTS]
         nc.gpsimd.tensor_tensor(out=a_hot[:], in0=ident[:, 0:32], in1=ident[:, 32:64], op=ADD)
         nc.gpsimd.tensor_tensor(out=c_hot[:], in0=ident[:, 64:96], in1=ident[:, 96:128], op=ADD)
@@ -361,25 +367,27 @@ def tile_differentiablelogicmachine_pa_k_kernel(tc, x1, x2, W2_words, W2_scales,
             multiply_order(g, AS_LIES)
             multiply_order(g, SWAPPED)
 
-        banks = [transpose_x2(word_planes(g)) for g in range(RUN)]
-        for g in range(RUN):
+        def warm_up(count):
+            for n in range(count):
+                nc.tensor.matmul(idle[:], lhsT=half_tile[:], rhs=zero_row[:], start=True, stop=True)
+
+        idle = y_acc[LAST_TILE]
+        warm_up(WARM_BEFORE)
+        banks = [transpose_x2(word_planes(0))]
+        warm_up(WARM_BETWEEN)
+        banks.append(transpose_x2(word_planes(1)))
+        warm_up(WARM_AFTER)
+        for g in range(2):
             prepare_x2(g, banks[g])
         multiply_all(0)
-        for run in range(1, PASSES // RUN):
-            if run == 1:
-                multiply_order(run * RUN - 1, AS_LIES)
-            banks = [transpose_x2(word_planes(run * RUN + g)) for g in range(RUN)]
-            for g in range(RUN):
-                prepare_x2(run * RUN + g, banks[g])
-            if run == X1_WITH_RUN:
+        for g in range(2, PASSES - 1):
+            prepare_x2(g, transpose_x2(word_planes(g)))
+            if g == X1_WITH_PASS:
                 regroup_x1(*transpose_x1_and_spread_bias())
-            if run == 1:
-                multiply_order(run * RUN - 1, SWAPPED)
-                multiply_all(run * RUN)
-            elif run < PASSES // RUN - 1:
-                multiply_all(run * RUN - 1)
-                multiply_all(run * RUN)
+            if g < PASSES - RUN:
+                multiply_all(g - 1)
         split_terms(multiply_x1())
+        prepare_x2(PASSES - 1, transpose_x2(word_planes(PASSES - 1)))
         multiply_all(PASSES - RUN - 1)
         spread = spread_terms()
         for t in range(LAST_TILE):

@@ -41,7 +41,7 @@ SCALE_RUNS = ((0, 2), (2, 4), (4, 8))
 WARM_BEFORE = 7
 WARM_BETWEEN = 2
 WARM_AFTER = 4
-PIECES = 4
+SORTED_BY_VECTOR = (4, 6)
 LAST_TILE = ROW_TILES - 1
 X1_WITH_PASS = 4
 
@@ -171,18 +171,25 @@ def tile_differentiablelogicmachine_pa_k_kernel(tc, x1, x2, W2_words, W2_scales,
         load_x2_words(2)
         load_scale_rows(3, 2)
         load_x2_later(3)
-        load_scale_rows(0, 0)
-        load_words(0, PASSES)
-        load_scale_rows(2, 0)
-        load_words(2 * PASSES, PASSES)
         load_x2_words(3)
+        for section in X1_SECTION:
+            load_scale_rows(section, 0)
+            for half in range(2):
+                load_words(section * PASSES + half * PASSES // 2, PASSES // 2)
 
         def word_planes(g):
+            return lambda t, u: first_words[:, g, t, u:WORDS_OF_PASS:2]
+
+        def sort_x2(g):
             if g < SINGLE:
-                return lambda t, u: first_words[:, g, t, u:WORDS_OF_PASS:2]
-            words = x2_later[g // RUN][:].bitcast(F32)
-            first = (g % RUN) * WORDS_OF_PASS
-            return lambda t, u: words[:, t, first + u : first + WORDS_OF_PASS : 2]
+                words = first_words[:, g, :, :]
+            else:
+                cols = slice((g % RUN) * WORDS_OF_PASS, (g % RUN + 1) * WORDS_OF_PASS)
+                words = x2_later[g // RUN][:].bitcast(F32)[:, :, cols]
+            ordered = stage.tile([P, ROW_TILES, 2, P], F32, name="ordered")
+            copy = nc.vector.tensor_copy if g in SORTED_BY_VECTOR else nc.scalar.copy
+            copy(out=ordered[:], in_=words.rearrange("p t (w u) -> p t u w", u=2))
+            return lambda t, u: ordered[:, t, u, :]
 
         def transpose_x2(planes):
             banks = []
@@ -241,14 +248,13 @@ def tile_differentiablelogicmachine_pa_k_kernel(tc, x1, x2, W2_words, W2_scales,
 
         def multiply_x2(t, g, orders=(AS_LIES, SWAPPED)):
             cols = slice(t * P, (t + 1) * P)
-            last_pass = PASSES - RUN - 1 if t == LAST_TILE else PASSES - 1
             for order in orders:
                 nc.tensor.matmul_mx(
                     out=y_acc[t][:],
                     lhsT=x2_codes[:, order, g, cols].bitcast(FP8X4),
                     lhsT_scale=x2_scales[:, order, g, cols],
                     start=(g == 0 and order == AS_LIES),
-                    stop=(g == last_pass and order == SWAPPED),
+                    stop=(g == PASSES - 1 and order == SWAPPED),
                     **weight(X2_SECTION[order], g),
                 )
 
@@ -309,55 +315,27 @@ def tile_differentiablelogicmachine_pa_k_kernel(tc, x1, x2, W2_words, W2_scales,
                 out=terms_split[:], in0=terms_high[:], scalar=low_rows[:], in1=terms[:], op0=MULT, op1=SUBTRACT
             )
 
-        def spread_terms():
-            spread = []
-            for t in range(ROW_TILES):
-                bank = work.tile([P, OUT], F32, tag="work", name="spread")
-                nc.tensor.matmul(bank[:], lhsT=hot[:, t * P : (t + 1) * P], rhs=terms_split[:], start=True, stop=True)
-                minus_terms = stage.tile([P, OUT], F32, bufs=ROW_TILES, name="minus_terms")
-                copy = nc.scalar.copy if t % 2 == 0 else nc.vector.tensor_copy
-                copy(out=minus_terms[:], in_=bank[:])
-                spread.append(minus_terms)
-            return spread
+        def spread_terms(t):
+            bank = work.tile([P, OUT], F32, tag="work", name="spread")
+            nc.tensor.matmul(bank[:], lhsT=hot[:, t * P : (t + 1) * P], rhs=terms_split[:], start=True, stop=True)
+            return bank
 
         out_by_tile = out.rearrange("b i j o -> (b i j) o").rearrange("(t p) o -> t p o", p=P)
 
-        def finish(t, minus_terms):
-            joined = stage.tile([P, OUT], F32, bufs=ROW_TILES, name="joined")
-            nc.vector.tensor_tensor(out=joined[:], in0=y_acc[t][:], in1=minus_terms[:], op=SUBTRACT)
-            result = stage.tile([P, OUT], F32, bufs=ROW_TILES, name="result")
-            nc.scalar.activation(out=result[:], in_=joined[:], func=SIGMOID)
-            nc.sync.dma_start(out=out_by_tile[t], in_=result[:])
+        def copy_sum(t):
+            y_sum = stage.tile([P, OUT], F32, bufs=ROW_TILES, name="y_sum")
+            nc.scalar.copy(out=y_sum[:], in_=y_acc[t][:])
+            return y_sum
 
-        def multiply_piece(piece):
-            width = OUT // PIECES
-            bank = work.tile([P, width], F32, tag="work", name="piece")
-            cols = slice(LAST_TILE * P, PAIRS)
-            for g in range(PASSES - RUN, PASSES):
-                for order in (AS_LIES, SWAPPED):
-                    nc.tensor.matmul_mx(
-                        out=bank[:],
-                        lhsT=x2_codes[:, order, g, cols].bitcast(FP8X4),
-                        lhsT_scale=x2_scales[:, order, g, cols],
-                        start=(g == PASSES - RUN and order == AS_LIES),
-                        stop=(g == PASSES - 1 and order == SWAPPED),
-                        **weight(X2_SECTION[order], g, piece * width, width),
-                    )
-            return bank
-
-        def join_last(minus_terms):
-            joined = stage.tile([P, OUT], F32, bufs=ROW_TILES, name="joined")
-            nc.vector.tensor_tensor(out=joined[:], in0=y_acc[LAST_TILE][:], in1=minus_terms[:], op=SUBTRACT)
-            return joined
-
-        def finish_piece(piece, bank, joined):
-            width = OUT // PIECES
-            cols = slice(piece * width, (piece + 1) * width)
-            whole = stage.tile([P, width], F32, bufs=PIECES, name="whole")
-            nc.vector.tensor_tensor(out=whole[:], in0=bank[:], in1=joined[:, cols], op=ADD)
-            result = stage.tile([P, width], F32, bufs=PIECES, name="piece_result")
-            nc.scalar.activation(out=result[:], in_=whole[:], func=SIGMOID)
-            nc.sync.dma_start(out=out_by_tile[LAST_TILE][:, cols], in_=result[:])
+        def finish(t, bank, y_sum):
+            parts = 2 if t == LAST_TILE else 1
+            for part in range(parts):
+                cols = slice(part * OUT // parts, (part + 1) * OUT // parts)
+                joined = stage.tile([P, OUT // parts], F32, bufs=ROW_TILES + 1, name="joined")
+                nc.vector.tensor_tensor(out=joined[:], in0=bank[:, cols], in1=y_sum[:, cols], op=SUBTRACT)
+                result = stage.tile([P, OUT // parts], F32, bufs=ROW_TILES + 1, name="result")
+                nc.scalar.activation(out=result[:], in_=joined[:], func=SIGMOID, scale=-1.0)
+                nc.sync.dma_start(out=out_by_tile[t][:, cols], in_=result[:])
 
         def multiply_order(g, order):
             for t in range(ROW_TILES):
@@ -377,24 +355,24 @@ def tile_differentiablelogicmachine_pa_k_kernel(tc, x1, x2, W2_words, W2_scales,
         warm_up(WARM_BETWEEN)
         banks.append(transpose_x2(word_planes(1)))
         warm_up(WARM_AFTER)
-        for g in range(2):
+        planes = {}
+        for g in range(RUN):
             prepare_x2(g, banks[g])
+        for g in range(RUN, 2 * RUN):
+            planes[g] = sort_x2(g)
         multiply_all(0)
-        for g in range(2, PASSES - 1):
-            prepare_x2(g, transpose_x2(word_planes(g)))
+        for g in range(RUN, PASSES):
+            prepare_x2(g, transpose_x2(planes[g]))
+            if g + RUN < PASSES:
+                planes[g + RUN] = sort_x2(g + RUN)
             if g == X1_WITH_PASS:
                 regroup_x1(*transpose_x1_and_spread_bias())
-            if g < PASSES - RUN:
-                multiply_all(g - 1)
+            multiply_all(g - 1)
         split_terms(multiply_x1())
-        prepare_x2(PASSES - 1, transpose_x2(word_planes(PASSES - 1)))
-        multiply_all(PASSES - RUN - 1)
-        spread = spread_terms()
-        for t in range(LAST_TILE):
-            for g in range(PASSES - RUN, PASSES):
-                multiply_x2(t, g)
-            finish(t, spread[t])
-            if t == 0:
-                joined = join_last(spread[LAST_TILE])
-        for piece in range(PIECES):
-            finish_piece(piece, multiply_piece(piece), joined)
+        sums_of_tiles = []
+        for t in range(ROW_TILES):
+            multiply_x2(t, PASSES - 1)
+            sums_of_tiles.append(copy_sum(t))
+        banks = [spread_terms(t) for t in range(ROW_TILES)]
+        for t in range(ROW_TILES):
+            finish(t, banks[t], sums_of_tiles[t])

@@ -36,14 +36,14 @@ SWAPPED = 1
 X2_SECTION = (1, 3)
 X1_SECTION = (0, 2)
 RUN = 2
-SINGLE = 2 * RUN
+BY_SCENE = (0, 1)
 SCALE_RUNS = ((0, 2), (2, 4), (4, 8))
 WARM_BEFORE = 7
 WARM_BETWEEN = 2
 WARM_AFTER = 4
-SORTED_BY_VECTOR = (4, 6)
+SORTED_BY_VECTOR = (2, 4, 6)
 LAST_TILE = ROW_TILES - 1
-X1_WITH_PASS = 4
+X1_WITH_PASS = 6
 
 FLOPS = 2 * PAIRS * SECTIONS * CHANNELS * OUT
 
@@ -57,11 +57,9 @@ def tile_differentiablelogicmachine_pa_k_kernel(tc, x1, x2, W2_words, W2_scales,
         work = ctx.enter_context(tc.psum_pool(name="work", bufs=4))
         ctx.enter_context(tc.manual_schedule())
 
-        x2_first = keep.tile([P, SINGLE, ROW_TILES, K_PASS], BF16)
-        x2_later = {
-            run: keep.tile([P, ROW_TILES, RUN * K_PASS], BF16, name="x2_later%d" % run)
-            for run in range(SINGLE // RUN, PASSES // RUN)
-        }
+        x2_runs = [
+            keep.tile([P, ROW_TILES, RUN * K_PASS], BF16, name="x2_run%d" % run) for run in range(PASSES // RUN)
+        ]
         x1_sb = keep.tile([P, CHANNELS // X1_PARTS], BF16)
         w_words = keep.tile([P, SECTIONS * PASSES, 2 * OUT], U8, align_bytes=64)
         scale_runs = {s: SCALE_RUNS if s in X2_SECTION else ((0, PASSES),) for s in range(SECTIONS)}
@@ -92,7 +90,6 @@ def tile_differentiablelogicmachine_pa_k_kernel(tc, x1, x2, W2_words, W2_scales,
         terms_split = keep.tile([P, OUT], BF16)
         y_acc = [sums.tile([P, OUT], F32, name="y_acc%d" % t) for t in range(ROW_TILES)]
 
-        first_words = x2_first[:].bitcast(F32)
         x1_words = x1_sb[:].bitcast(F32)
 
         make_identity(nc, ident[:])
@@ -127,9 +124,12 @@ def tile_differentiablelogicmachine_pa_k_kernel(tc, x1, x2, W2_words, W2_scales,
         words_dram = W2_words.bitcast(I32).rearrange("g p n -> p g n")
         scales_dram = W2_scales.bitcast(I32).rearrange("g (q r) n -> r q g n", r=4)
 
-        def load_x2_later(run):
+        def load_x2(run):
             cols = slice(run * RUN * K_PASS, (run + 1) * RUN * K_PASS)
-            nc.sync.dma_start(out=x2_later[run][:], in_=x2_by_tile[:, :, cols])
+            pieces = SCENES if run in BY_SCENE else 1
+            for piece in range(pieces):
+                tiles = slice(piece * ROW_TILES // pieces, (piece + 1) * ROW_TILES // pieces)
+                nc.sync.dma_start(out=x2_runs[run][:, tiles, :], in_=x2_by_tile[:, tiles, cols])
 
         def load_words(first_pass, passes):
             span = slice(first_pass, first_pass + passes)
@@ -147,72 +147,62 @@ def tile_differentiablelogicmachine_pa_k_kernel(tc, x1, x2, W2_words, W2_scales,
             for section in X2_SECTION:
                 load_words(section * PASSES + run * RUN, RUN)
 
-        def load_x2_first(g, halves):
-            for half in range(halves):
-                tiles = slice(half * ROW_TILES // halves, (half + 1) * ROW_TILES // halves)
-                nc.sync.dma_start(
-                    out=x2_first[:, g, tiles, :], in_=x2_by_tile[:, tiles, g * K_PASS : (g + 1) * K_PASS]
-                )
-
-        load_x2_first(0, 2)
-        load_x2_first(1, 1)
+        load_x2(0)
         load_scale_rows(1, 0)
         load_x2_words(0)
         load_scale_rows(3, 0)
-        load_x2_first(2, 1)
+        load_x2(1)
         load_scale_rows(1, 1)
-        load_x2_first(3, 1)
-        load_scale_rows(3, 1)
         load_x2_words(1)
-        nc.sync.dma_start(out=x1_sb[:], in_=x1.rearrange("b n (c k) -> (b n c) k", c=X1_PARTS))
-        nc.sync.dma_start(out=bias_row[0:1, :], in_=b2.rearrange("(m o) -> m o", m=1))
-        load_x2_later(2)
+        load_scale_rows(3, 1)
+        load_x2(2)
         load_scale_rows(1, 2)
         load_x2_words(2)
         load_scale_rows(3, 2)
-        load_x2_later(3)
+        load_x2(3)
+        nc.sync.dma_start(out=x1_sb[:], in_=x1.rearrange("b n (c k) -> (b n c) k", c=X1_PARTS))
+        nc.sync.dma_start(out=bias_row[0:1, :], in_=b2.rearrange("(m o) -> m o", m=1))
         load_x2_words(3)
         for section in X1_SECTION:
             load_scale_rows(section, 0)
             for half in range(2):
                 load_words(section * PASSES + half * PASSES // 2, PASSES // 2)
 
+        def words_of(g):
+            first = (g % RUN) * WORDS_OF_PASS
+            return x2_runs[g // RUN][:].bitcast(F32)[:, :, first : first + WORDS_OF_PASS]
+
         def word_planes(g):
-            return lambda t, u: first_words[:, g, t, u:WORDS_OF_PASS:2]
+            words = words_of(g)
+            return lambda t, u: words[:, t, u:WORDS_OF_PASS:2]
 
         def sort_x2(g):
-            if g < SINGLE:
-                words = first_words[:, g, :, :]
-            else:
-                cols = slice((g % RUN) * WORDS_OF_PASS, (g % RUN + 1) * WORDS_OF_PASS)
-                words = x2_later[g // RUN][:].bitcast(F32)[:, :, cols]
             ordered = stage.tile([P, ROW_TILES, 2, P], F32, name="ordered")
             copy = nc.vector.tensor_copy if g in SORTED_BY_VECTOR else nc.scalar.copy
-            copy(out=ordered[:], in_=words.rearrange("p t (w u) -> p t u w", u=2))
+            copy(out=ordered[:], in_=words_of(g).rearrange("p t (w u) -> p t u w", u=2))
             return lambda t, u: ordered[:, t, u, :]
 
-        def transpose_x2(planes):
-            banks = []
-            for scene in range(SCENES):
-                xt = work.tile([P, 2, PAIRS_OF_SCENE], F32, tag="work", name="xt")
-                for u in range(2):
-                    for half in range(2):
-                        nc.tensor.transpose(
-                            xt[:, u, half * P : (half + 1) * P],
-                            planes(2 * scene + half, u),
-                            ident[:],
-                        )
-                banks.append(xt)
-            return banks
+        def transpose_scene(planes, scene):
+            xt = work.tile([P, 2, PAIRS_OF_SCENE], F32, tag="work", name="xt")
+            for u in range(2):
+                for half in range(2):
+                    nc.tensor.transpose(
+                        xt[:, u, half * P : (half + 1) * P],
+                        planes(2 * scene + half, u),
+                        ident[:],
+                    )
+            return xt
 
-        def regroup_x2(g, banks):
-            grouped = stage.tile([P, PAIRS, 4], BF16, align_bytes=64)
-            grouped_words = grouped[:].bitcast(F32)
-            for scene in range(SCENES):
-                cols = slice(scene * PAIRS_OF_SCENE, (scene + 1) * PAIRS_OF_SCENE)
-                copy = nc.vector.tensor_copy if (g <= RUN and scene == 1) else nc.scalar.copy
-                copy(out=grouped_words[:, cols, :], in_=banks[scene][:].rearrange("p u r -> p r u"))
+        def transpose_x2(planes):
+            return [transpose_scene(planes, scene) for scene in range(SCENES)]
+
+        def new_grouped():
+            grouped = stage.tile([P, PAIRS, 4], BF16, align_bytes=64, name="grouped")
             return grouped
+
+        def regroup_scene(grouped, scene, bank, copy):
+            cols = slice(scene * PAIRS_OF_SCENE, (scene + 1) * PAIRS_OF_SCENE)
+            copy(out=grouped[:].bitcast(F32)[:, cols, :], in_=bank[:].rearrange("p u r -> p r u"))
 
         def quantise_x2(g, grouped, first_scene, scenes):
             cols = slice(first_scene * PAIRS_OF_SCENE, (first_scene + scenes) * PAIRS_OF_SCENE)
@@ -230,12 +220,11 @@ def tile_differentiablelogicmachine_pa_k_kernel(tc, x1, x2, W2_words, W2_scales,
                 )
 
         def prepare_x2(g, banks):
-            grouped = regroup_x2(g, banks)
-            if g == 0:
-                for scene in range(SCENES):
-                    quantise_x2(g, grouped, scene, 1)
-            else:
-                quantise_x2(g, grouped, 0, SCENES)
+            grouped = new_grouped()
+            for scene in range(SCENES):
+                copy = nc.vector.tensor_copy if (g == RUN and scene == 1) else nc.scalar.copy
+                regroup_scene(grouped, scene, banks[scene], copy)
+            quantise_x2(g, grouped, 0, SCENES)
             swap_x2(g)
 
         def weight(section, g, first=0, width=OUT):
@@ -351,23 +340,29 @@ def tile_differentiablelogicmachine_pa_k_kernel(tc, x1, x2, W2_words, W2_scales,
 
         idle = y_acc[LAST_TILE]
         warm_up(WARM_BEFORE)
-        banks = [transpose_x2(word_planes(0))]
-        warm_up(WARM_BETWEEN)
-        banks.append(transpose_x2(word_planes(1)))
-        warm_up(WARM_AFTER)
-        planes = {}
-        for g in range(RUN):
-            prepare_x2(g, banks[g])
-        for g in range(RUN, 2 * RUN):
-            planes[g] = sort_x2(g)
+        grouped = [new_grouped() for g in range(RUN)]
+        for scene in range(SCENES):
+            banks = [transpose_scene(word_planes(g), scene) for g in range(RUN)]
+            warm_up(WARM_BETWEEN if scene == 0 else WARM_AFTER)
+            for g in range(RUN):
+                regroup_scene(grouped[g], scene, banks[g], nc.scalar.copy)
+            quantise_x2(0, grouped[0], scene, 1)
+        swap_x2(0)
+        quantise_x2(1, grouped[1], 0, SCENES)
+        swap_x2(1)
+        planes = {g: sort_x2(g) for g in range(RUN, 2 * RUN)}
         multiply_all(0)
+        multiply_order(1, AS_LIES)
         for g in range(RUN, PASSES):
             prepare_x2(g, transpose_x2(planes[g]))
             if g + RUN < PASSES:
                 planes[g + RUN] = sort_x2(g + RUN)
             if g == X1_WITH_PASS:
                 regroup_x1(*transpose_x1_and_spread_bias())
-            multiply_all(g - 1)
+            if g == RUN:
+                multiply_order(1, SWAPPED)
+            else:
+                multiply_all(g - 1)
         split_terms(multiply_x1())
         sums_of_tiles = []
         for t in range(ROW_TILES):

@@ -162,11 +162,11 @@ def tile_differentiablelogicmachine_pa_k_kernel(tc, x1, x2, W2_words, W2_scales,
         load_x2(3)
         nc.sync.dma_start(out=x1_sb[:], in_=x1.rearrange("b n (c k) -> (b n c) k", c=X1_PARTS))
         nc.sync.dma_start(out=bias_row[0:1, :], in_=b2.rearrange("(m o) -> m o", m=1))
-        load_x2_words(3)
         for section in X1_SECTION:
             load_scale_rows(section, 0)
             for half in range(2):
                 load_words(section * PASSES + half * PASSES // 2, PASSES // 2)
+        load_x2_words(3)
 
         def words_of(g):
             first = (g % RUN) * WORDS_OF_PASS
@@ -311,19 +311,19 @@ def tile_differentiablelogicmachine_pa_k_kernel(tc, x1, x2, W2_words, W2_scales,
 
         out_by_tile = out.rearrange("b i j o -> (b i j) o").rearrange("(t p) o -> t p o", p=P)
 
-        def copy_sum(t):
-            y_sum = stage.tile([P, OUT], F32, bufs=ROW_TILES, name="y_sum")
-            nc.scalar.copy(out=y_sum[:], in_=y_acc[t][:])
-            return y_sum
+        def copy_out(bank, copy):
+            copied = stage.tile([P, OUT], F32, bufs=ROW_TILES, name="copied")
+            copy(out=copied[:], in_=bank[:])
+            return copied
 
-        def finish(t, bank, y_sum):
+        def finish(t, minuend, subtrahend, sign):
             parts = 2 if t == LAST_TILE else 1
             for part in range(parts):
                 cols = slice(part * OUT // parts, (part + 1) * OUT // parts)
                 joined = stage.tile([P, OUT // parts], F32, bufs=ROW_TILES + 1, name="joined")
-                nc.vector.tensor_tensor(out=joined[:], in0=bank[:, cols], in1=y_sum[:, cols], op=SUBTRACT)
+                nc.vector.tensor_tensor(out=joined[:], in0=minuend[:, cols], in1=subtrahend[:, cols], op=SUBTRACT)
                 result = stage.tile([P, OUT // parts], F32, bufs=ROW_TILES + 1, name="result")
-                nc.scalar.activation(out=result[:], in_=joined[:], func=SIGMOID, scale=-1.0)
+                nc.scalar.activation(out=result[:], in_=joined[:], func=SIGMOID, scale=sign)
                 nc.sync.dma_start(out=out_by_tile[t][:, cols], in_=result[:])
 
         def multiply_order(g, order):
@@ -333,6 +333,10 @@ def tile_differentiablelogicmachine_pa_k_kernel(tc, x1, x2, W2_words, W2_scales,
         def multiply_all(g):
             multiply_order(g, AS_LIES)
             multiply_order(g, SWAPPED)
+
+        def close_tile(t):
+            for g in range(PASSES - RUN, PASSES):
+                multiply_x2(t, g)
 
         def warm_up(count):
             for n in range(count):
@@ -354,20 +358,26 @@ def tile_differentiablelogicmachine_pa_k_kernel(tc, x1, x2, W2_words, W2_scales,
         multiply_all(0)
         multiply_order(1, AS_LIES)
         for g in range(RUN, PASSES):
-            prepare_x2(g, transpose_x2(planes[g]))
-            if g + RUN < PASSES:
-                planes[g + RUN] = sort_x2(g + RUN)
+            banks = transpose_x2(planes[g])
             if g == X1_WITH_PASS:
                 regroup_x1(*transpose_x1_and_spread_bias())
+            prepare_x2(g, banks)
+            if g + RUN < PASSES:
+                planes[g + RUN] = sort_x2(g + RUN)
             if g == RUN:
                 multiply_order(1, SWAPPED)
-            else:
+            elif g < PASSES - 1:
                 multiply_all(g - 1)
         split_terms(multiply_x1())
         sums_of_tiles = []
-        for t in range(ROW_TILES):
-            multiply_x2(t, PASSES - 1)
-            sums_of_tiles.append(copy_sum(t))
+        for t in (0, 1):
+            close_tile(t)
+            sums_of_tiles.append(copy_out(y_acc[t], nc.scalar.copy))
         banks = [spread_terms(t) for t in range(ROW_TILES)]
-        for t in range(ROW_TILES):
-            finish(t, banks[t], sums_of_tiles[t])
+        spreads = {2: copy_out(banks[2], nc.scalar.copy)}
+        for t in (0, 1):
+            finish(t, banks[t], sums_of_tiles[t], -1.0)
+        spreads[3] = copy_out(banks[3], nc.vector.tensor_copy)
+        for t in (2, 3):
+            close_tile(t)
+            finish(t, y_acc[t], spreads[t], 1.0)

@@ -38,9 +38,10 @@ X1_SECTION = (0, 2)
 RUN = 2
 BY_SCENE = (0, 1)
 SCALE_RUNS = ((0, 2), (2, 4), (4, 8))
+X1_WORD_PIECES = (((0, 4), (4, 8)), ((0, 4), (4, 6), (6, 8)))
 WARM_BEFORE = 7
-WARM_BETWEEN = 2
-WARM_AFTER = 4
+WARM_BETWEEN = 1
+WARM_AFTER = 1
 SORTED_BY_VECTOR = (2, 4, 6)
 LAST_TILE = ROW_TILES - 1
 X1_WITH_PASS = 6
@@ -96,11 +97,11 @@ def tile_differentiablelogicmachine_pa_k_kernel(tc, x1, x2, W2_words, W2_scales,
         nc.vector.memset(half_tile[:], 0.5)
         nc.vector.memset(zero_row[:].bitcast(I32), 0)
         nc.vector.memset(table_warm[:], 0.0)
+        nc.vector.memset(bias_row[:].bitcast(I32), 0)
         for section, runs in scale_runs.items():
             if section in X2_SECTION:
                 for first, end in runs:
                     nc.vector.memset(w_scales[section, first][:].bitcast(I32), 0)
-        nc.vector.memset(bias_row[:].bitcast(I32), 0)
         for section in X1_SECTION:
             nc.vector.memset(w_scales[section, 0][:].bitcast(I32), 0)
         nc.vector.memset(x1_codes[:, PASSES * P :], 0)
@@ -148,6 +149,7 @@ def tile_differentiablelogicmachine_pa_k_kernel(tc, x1, x2, W2_words, W2_scales,
                 load_words(section * PASSES + run * RUN, RUN)
 
         load_x2(0)
+        nc.sync.dma_start(out=bias_row[0:1, :], in_=b2.rearrange("(m o) -> m o", m=1))
         load_scale_rows(1, 0)
         load_x2_words(0)
         load_scale_rows(3, 0)
@@ -161,11 +163,10 @@ def tile_differentiablelogicmachine_pa_k_kernel(tc, x1, x2, W2_words, W2_scales,
         load_scale_rows(3, 2)
         load_x2(3)
         nc.sync.dma_start(out=x1_sb[:], in_=x1.rearrange("b n (c k) -> (b n c) k", c=X1_PARTS))
-        nc.sync.dma_start(out=bias_row[0:1, :], in_=b2.rearrange("(m o) -> m o", m=1))
-        for section in X1_SECTION:
+        for section, pieces in zip(X1_SECTION, X1_WORD_PIECES):
             load_scale_rows(section, 0)
-            for half in range(2):
-                load_words(section * PASSES + half * PASSES // 2, PASSES // 2)
+            for first, end in pieces:
+                load_words(section * PASSES + first, end - first)
         load_x2_words(3)
 
         def words_of(g):
@@ -212,11 +213,12 @@ def tile_differentiablelogicmachine_pa_k_kernel(tc, x1, x2, W2_words, W2_scales,
                 in_=grouped[:, cols, :].rearrange("p r t -> p (r t)"),
             )
 
-        def swap_x2(g):
+        def swap_x2(g, first_scene, scenes):
+            cols = slice(first_scene * PAIRS_OF_SCENE, (first_scene + scenes) * PAIRS_OF_SCENE)
             for plane in (x2_codes[:].bitcast(I32), x2_scales[:]):
                 nc.vector.tensor_copy(
-                    out=plane[:, SWAPPED, g, :].rearrange("p (b q r j) -> p b q j r", b=SCENES, q=4, r=4),
-                    in_=plane[:, AS_LIES, g, :].rearrange("p (b j q r) -> p b q j r", b=SCENES, q=4, r=4),
+                    out=plane[:, SWAPPED, g, cols].rearrange("p (b q r j) -> p b q j r", b=scenes, q=4, r=4),
+                    in_=plane[:, AS_LIES, g, cols].rearrange("p (b j q r) -> p b q j r", b=scenes, q=4, r=4),
                 )
 
         def prepare_x2(g, banks):
@@ -225,7 +227,7 @@ def tile_differentiablelogicmachine_pa_k_kernel(tc, x1, x2, W2_words, W2_scales,
                 copy = nc.vector.tensor_copy if (g == RUN and scene == 1) else nc.scalar.copy
                 regroup_scene(grouped, scene, banks[scene], copy)
             quantise_x2(g, grouped, 0, SCENES)
-            swap_x2(g)
+            swap_x2(g, 0, SCENES)
 
         def weight(section, g, first=0, width=OUT):
             w_pass = section * PASSES + g
@@ -247,7 +249,12 @@ def tile_differentiablelogicmachine_pa_k_kernel(tc, x1, x2, W2_words, W2_scales,
                     **weight(X2_SECTION[order], g),
                 )
 
-        def transpose_x1_and_spread_bias():
+        def spread_bias():
+            bias_all = work.tile([P, OUT], F32, tag="work", name="bias_all")
+            nc.tensor.matmul(bias_all[:], lhsT=half_tile[:], rhs=bias_row[:], start=True, stop=True)
+            return bias_all
+
+        def transpose_x1():
             x1t = work.tile([P, 2, 2, P], F32, tag="work", name="x1t")
             for local in range(2):
                 first_word = local * WORDS_OF_PASS
@@ -257,11 +264,9 @@ def tile_differentiablelogicmachine_pa_k_kernel(tc, x1, x2, W2_words, W2_scales,
                         x1_words[:, first_word + u : first_word + WORDS_OF_PASS : 2],
                         ident[:],
                     )
-            bias_all = work.tile([P, OUT], F32, tag="work", name="bias_all")
-            nc.tensor.matmul(bias_all[:], lhsT=half_tile[:], rhs=bias_row[:], start=True, stop=True)
-            return x1t, bias_all
+            return x1t
 
-        def regroup_x1(x1t, bias_all):
+        def regroup_x1(x1t):
             by_part = x1_grouped[:].bitcast(F32).rearrange("p (c l) h (k n) u -> p l h k c n u", l=2, k=2)
             for local in range(2):
                 for copy_of_x1 in range(2):
@@ -269,7 +274,6 @@ def tile_differentiablelogicmachine_pa_k_kernel(tc, x1, x2, W2_words, W2_scales,
                         out=by_part[:, local, 1, copy_of_x1],
                         in_=x1t[:, local].rearrange("p u (r c) -> p c r u", c=X1_PARTS),
                     )
-            nc.scalar.copy(out=bias_half[:], in_=bias_all[:])
             nc.vector.quantize_mx(
                 out=x1_codes[:, 0 : PASSES * P].bitcast(FP8X4),
                 scales=x1_scales[:, 0 : PASSES * P],
@@ -334,9 +338,10 @@ def tile_differentiablelogicmachine_pa_k_kernel(tc, x1, x2, W2_words, W2_scales,
             multiply_order(g, AS_LIES)
             multiply_order(g, SWAPPED)
 
-        def close_tile(t):
-            for g in range(PASSES - RUN, PASSES):
-                multiply_x2(t, g)
+        def multiply_last(t, orders):
+            for order in orders:
+                for g in range(PASSES - RUN, PASSES):
+                    multiply_x2(t, g, (order,))
 
         def warm_up(count):
             for n in range(count):
@@ -347,20 +352,26 @@ def tile_differentiablelogicmachine_pa_k_kernel(tc, x1, x2, W2_words, W2_scales,
         grouped = [new_grouped() for g in range(RUN)]
         for scene in range(SCENES):
             banks = [transpose_scene(word_planes(g), scene) for g in range(RUN)]
+            if scene == 0:
+                bias_all = spread_bias()
             warm_up(WARM_BETWEEN if scene == 0 else WARM_AFTER)
             for g in range(RUN):
                 regroup_scene(grouped[g], scene, banks[g], nc.scalar.copy)
             quantise_x2(0, grouped[0], scene, 1)
-        swap_x2(0)
+            swap_x2(0, scene, 1)
+        nc.scalar.copy(out=bias_half[:], in_=bias_all[:])
         quantise_x2(1, grouped[1], 0, SCENES)
-        swap_x2(1)
+        swap_x2(1, 0, SCENES)
         planes = {g: sort_x2(g) for g in range(RUN, 2 * RUN)}
-        multiply_all(0)
+        for scene in range(SCENES):
+            for order in (AS_LIES, SWAPPED):
+                for t in range(2 * scene, 2 * scene + 2):
+                    multiply_x2(t, 0, (order,))
         multiply_order(1, AS_LIES)
         for g in range(RUN, PASSES):
             banks = transpose_x2(planes[g])
             if g == X1_WITH_PASS:
-                regroup_x1(*transpose_x1_and_spread_bias())
+                regroup_x1(transpose_x1())
             prepare_x2(g, banks)
             if g + RUN < PASSES:
                 planes[g + RUN] = sort_x2(g + RUN)
@@ -371,7 +382,9 @@ def tile_differentiablelogicmachine_pa_k_kernel(tc, x1, x2, W2_words, W2_scales,
         split_terms(multiply_x1())
         sums_of_tiles = []
         for t in (0, 1):
-            close_tile(t)
+            multiply_last(t, (AS_LIES,))
+        for t in (0, 1):
+            multiply_last(t, (SWAPPED,))
             sums_of_tiles.append(copy_out(y_acc[t], nc.scalar.copy))
         banks = [spread_terms(t) for t in range(ROW_TILES)]
         spreads = {2: copy_out(banks[2], nc.scalar.copy)}
@@ -379,5 +392,5 @@ def tile_differentiablelogicmachine_pa_k_kernel(tc, x1, x2, W2_words, W2_scales,
             finish(t, banks[t], sums_of_tiles[t], -1.0)
         spreads[3] = copy_out(banks[3], nc.vector.tensor_copy)
         for t in (2, 3):
-            close_tile(t)
+            multiply_last(t, (AS_LIES, SWAPPED))
             finish(t, y_acc[t], spreads[t], 1.0)

@@ -255,30 +255,35 @@ def tile_differentiablelogicmachine_pa_k_kernel(tc, x1, x2, W2_words, W2_scales,
             return bias_all
 
         def transpose_x1():
-            x1t = work.tile([P, 2, 2, P], F32, tag="work", name="x1t")
+            banks = []
             for local in range(2):
                 first_word = local * WORDS_OF_PASS
+                x1t = work.tile([P, 2, P], F32, tag="work", name="x1t")
                 for u in range(2):
                     nc.tensor.transpose(
-                        x1t[:, local, u, :],
+                        x1t[:, u, :],
                         x1_words[:, first_word + u : first_word + WORDS_OF_PASS : 2],
                         ident[:],
                     )
-            return x1t
+                banks.append(x1t)
+            return banks
 
-        def regroup_x1(x1t):
+        def regroup_x1(banks):
             by_part = x1_grouped[:].bitcast(F32).rearrange("p (c l) h (k n) u -> p l h k c n u", l=2, k=2)
-            for local in range(2):
-                for copy_of_x1 in range(2):
-                    nc.scalar.copy(
+            for copy_of_x1 in range(2):
+                for local, copy in enumerate((nc.scalar.copy, nc.vector.tensor_copy)):
+                    copy(
                         out=by_part[:, local, 1, copy_of_x1],
-                        in_=x1t[:, local].rearrange("p u (r c) -> p c r u", c=X1_PARTS),
+                        in_=banks[local][:].rearrange("p u (r c) -> p c r u", c=X1_PARTS),
                     )
-            nc.vector.quantize_mx(
-                out=x1_codes[:, 0 : PASSES * P].bitcast(FP8X4),
-                scales=x1_scales[:, 0 : PASSES * P],
-                in_=x1_grouped[:].rearrange("p g h n t -> p (g h n t)"),
-            )
+            for half in range(2):
+                passes = slice(half * PASSES // 2, (half + 1) * PASSES // 2)
+                cols = slice(passes.start * P, passes.stop * P)
+                nc.vector.quantize_mx(
+                    out=x1_codes[:, cols].bitcast(FP8X4),
+                    scales=x1_scales[:, cols],
+                    in_=x1_grouped[:, passes].rearrange("p g h n t -> p (g h n t)"),
+                )
             nc.vector.tensor_reduce(
                 out=low_rows[:],
                 in_=ident[:].rearrange("p (h q r) -> p h q r", h=2, q=2)[:, :, 1, :],

@@ -36,7 +36,7 @@ SWAPPED = 1
 X2_SECTION = (1, 3)
 X1_SECTION = (0, 2)
 RUN = 2
-BY_SCENE = (0, 1)
+BY_SCENE = (0,)
 SCALE_RUNS = ((0, 2), (2, 4), (4, 8))
 X1_WORD_PIECES = (((0, 4), (4, 8)), ((0, 4), (4, 6), (6, 8)))
 WARM_BEFORE = 7
@@ -307,11 +307,20 @@ def tile_differentiablelogicmachine_pa_k_kernel(tc, x1, x2, W2_words, W2_scales,
             return ac
 
         def split_terms(ac):
-            nc.vector.tensor_tensor(out=terms[:], in0=ac[:], in1=bias_half[:], op=ADD)
-            nc.vector.tensor_copy(out=terms_high[:], in_=terms[:])
-            nc.vector.scalar_tensor_tensor(
-                out=terms_split[:], in0=terms_high[:], scalar=low_rows[:], in1=terms[:], op0=MULT, op1=SUBTRACT
-            )
+            halves = [slice(half * OUT // 2, (half + 1) * OUT // 2) for half in range(2)]
+            for cols in halves:
+                nc.vector.tensor_tensor(out=terms[:, cols], in0=ac[:, cols], in1=bias_half[:, cols], op=ADD)
+            for cols in halves:
+                nc.vector.tensor_copy(out=terms_high[:, cols], in_=terms[:, cols])
+            for cols in halves:
+                nc.vector.scalar_tensor_tensor(
+                    out=terms_split[:, cols],
+                    in0=terms_high[:, cols],
+                    scalar=low_rows[:],
+                    in1=terms[:, cols],
+                    op0=MULT,
+                    op1=SUBTRACT,
+                )
 
         def spread_terms(t):
             bank = work.tile([P, OUT], F32, tag="work", name="spread")

from contextlib import ExitStack

import concourse.mybir as mybir
from concourse.masks import make_identity

F32 = mybir.dt.float32
BF16 = mybir.dt.bfloat16
I32 = mybir.dt.int32
U32 = mybir.dt.uint32
U8 = mybir.dt.uint8
FP8X4 = mybir.dt.float8_e4m3fn_x4
FP4X4 = mybir.dt.float4_e2m1fn_x4
ADD = mybir.AluOpType.add
SUBTRACT = mybir.AluOpType.subtract
MULT = mybir.AluOpType.mult
SIGMOID = mybir.ActivationFunctionType.Sigmoid
AXES_XY = mybir.AxisListType.XY

P = 128
SCENES = 2
OBJECTS = 16
CHANNELS = 4096
OUT = 512
PAIRS_OF_SCENE = OBJECTS * OBJECTS
PAIRS = SCENES * PAIRS_OF_SCENE
SINGLES = SCENES * OBJECTS
K_PASS = 4 * P
PASSES = CHANNELS // K_PASS
SECTIONS = 4
WORDS_OF_PASS = K_PASS // 2
ROW_TILES = PAIRS // P
X1_PARTS = P // SINGLES
HALF = P // 2
AS_LIES = 0
SWAPPED = 1
X2_SECTION = (1, 3)
X1_SECTION = (0, 2)
RUN = 2
BY_SCENE = (0,)
SCALE_RUNS = ((0, 2), (2, 4), (4, 8))
X1_WORD_PIECES = (((0, 4), (4, 8)), ((0, 4), (4, 6), (6, 8)))
WARM_BEFORE = 7
WARM_BETWEEN = 1
WARM_AFTER = 1
SORTED_BY_VECTOR = (2, 4, 6)
LAST_TILE = ROW_TILES - 1
X1_WITH_PASS = 6

FLOPS = 2 * PAIRS * SECTIONS * CHANNELS * OUT


def tile_differentiablelogicmachine_pa_k_kernel(tc, x1, x2, W2_words, W2_scales, b2, out):
    nc = tc.nc
    with ExitStack() as ctx:
        keep = ctx.enter_context(tc.tile_pool(name="keep", bufs=1))
        stage = ctx.enter_context(tc.tile_pool(name="stage", bufs=3))
        sums = ctx.enter_context(tc.psum_pool(name="sums", bufs=1))
        work = ctx.enter_context(tc.psum_pool(name="work", bufs=4))
        ctx.enter_context(tc.manual_schedule())

        x2_runs = [
            keep.tile([P, ROW_TILES, RUN * K_PASS], BF16, name="x2_run%d" % run) for run in range(PASSES // RUN)
        ]
        x1_sb = keep.tile([P, CHANNELS // X1_PARTS], BF16)
        w_words = keep.tile([P, SECTIONS * PASSES, 2 * OUT], U8, align_bytes=64)
        scale_runs = {s: SCALE_RUNS if s in X2_SECTION else ((0, PASSES),) for s in range(SECTIONS)}
        w_scales = {}
        for section, runs in scale_runs.items():
            for first, end in runs:
                w_scales[section, first] = keep.tile(
                    [P, end - first, OUT], U8, align_bytes=64, name="w_scales%d_%d" % (section, first)
                )
        x2_codes = keep.tile([P, 2, PASSES, PAIRS], U32, align_bytes=64)
        x2_scales = keep.tile([P, 2, PASSES, PAIRS], U8, align_bytes=64)
        x1_grouped = keep.tile([P, PASSES, 2, HALF, 4], BF16, align_bytes=64)
        x1_codes = keep.tile([P, PASSES * P + HALF], U32, align_bytes=64)
        x1_scales = keep.tile([P, PASSES * P + HALF], U8, align_bytes=64)
        ident = keep.tile([P, P], F32)
        a_hot = keep.tile([P, SINGLES], BF16)
        c_hot = keep.tile([P, SINGLES], BF16)
        hot = keep.tile([P, PAIRS], BF16)
        low_rows = keep.tile([P, 1], F32)
        bias_row = keep.tile([P, OUT], BF16)
        half_tile = keep.tile([P, P], BF16)
        zero_row = keep.tile([P, OUT], BF16)
        bias_half = keep.tile([P, OUT], F32)
        table_warm = keep.tile([P, 1], F32)
        sigmoid_warm = keep.tile([P, 1], F32)
        terms = keep.tile([P, OUT], F32)
        terms_high = keep.tile([P, OUT], BF16)
        terms_split = keep.tile([P, OUT], BF16)
        y_acc = [sums.tile([P, OUT], F32, name="y_acc%d" % t) for t in range(ROW_TILES)]

        x1_words = x1_sb[:].bitcast(F32)

        make_identity(nc, ident[:])
        nc.vector.memset(half_tile[:], 0.5)
        nc.vector.memset(zero_row[:].bitcast(I32), 0)
        nc.vector.memset(table_warm[:], 0.0)
        nc.vector.memset(bias_row[:].bitcast(I32), 0)
        for section, runs in scale_runs.items():
            if section in X2_SECTION:
                for first, end in runs:
                    nc.vector.memset(w_scales[section, first][:].bitcast(I32), 0)
        for section in X1_SECTION:
            nc.vector.memset(w_scales[section, 0][:].bitcast(I32), 0)
        nc.vector.memset(x1_codes[:, PASSES * P :], 0)
        nc.vector.memset(x1_scales[:, PASSES * P :].bitcast(I32), 0)
        nc.scalar.copy(
            out=x1_grouped[:].bitcast(F32)[:, :, 0, :, :].rearrange("p g n u -> p g (n u)"),
            in_=table_warm[:].unsqueeze(2).to_broadcast([P, PASSES, 2 * HALF]),
        )
        nc.scalar.activation(out=sigmoid_warm[:], in_=table_warm[:], func=SIGMOID)
        pair_shape = [P, SCENES, OBJECTS, OBJECTS]
        nc.gpsimd.tensor_tensor(out=a_hot[:], in0=ident[:, 0:32], in1=ident[:, 32:64], op=ADD)
        nc.gpsimd.tensor_tensor(out=c_hot[:], in0=ident[:, 64:96], in1=ident[:, 96:128], op=ADD)
        nc.gpsimd.tensor_tensor(
            out=hot[:].rearrange("p (b i j) -> p b i j", b=SCENES, i=OBJECTS),
            in0=a_hot[:].rearrange("p (b i) -> p b i", b=SCENES).unsqueeze(3).to_broadcast(pair_shape),
            in1=c_hot[:].rearrange("p (b j) -> p b j", b=SCENES).unsqueeze(2).to_broadcast(pair_shape),
            op=ADD,
        )

        x2_by_tile = x2.rearrange("b i j k -> (b i j) k").rearrange("(t p) k -> p t k", p=P)
        words_dram = W2_words.bitcast(I32).rearrange("g p n -> p g n")
        scales_dram = W2_scales.bitcast(I32).rearrange("g (q r) n -> r q g n", r=4)

        def load_x2(run):
            cols = slice(run * RUN * K_PASS, (run + 1) * RUN * K_PASS)
            pieces = SCENES if run in BY_SCENE else 1
            for piece in range(pieces):
                tiles = slice(piece * ROW_TILES // pieces, (piece + 1) * ROW_TILES // pieces)
                nc.sync.dma_start(out=x2_runs[run][:, tiles, :], in_=x2_by_tile[:, tiles, cols])

        def load_words(first_pass, passes):
            span = slice(first_pass, first_pass + passes)
            nc.sync.dma_start(out=w_words[:, span, :].bitcast(I32), in_=words_dram[:, span, :])

        def load_scale_rows(section, run):
            first, end = scale_runs[section][run]
            span = slice(section * PASSES + first, section * PASSES + end)
            for r in range(4):
                nc.sync.dma_start(
                    out=w_scales[section, first][r:P:32, :, :].bitcast(I32), in_=scales_dram[r, :, span, :]
                )

        def load_x2_words(run):
            for section in X2_SECTION:
                load_words(section * PASSES + run * RUN, RUN)

        load_x2(0)
        nc.sync.dma_start(out=bias_row[0:1, :], in_=b2.rearrange("(m o) -> m o", m=1))
        load_scale_rows(1, 0)
        load_x2_words(0)
        load_scale_rows(3, 0)
        load_x2(1)
        load_scale_rows(1, 1)
        load_x2_words(1)
        load_scale_rows(3, 1)
        load_x2(2)
        load_scale_rows(1, 2)
        load_x2_words(2)
        load_scale_rows(3, 2)
        load_x2(3)
        nc.sync.dma_start(out=x1_sb[:], in_=x1.rearrange("b n (c k) -> (b n c) k", c=X1_PARTS))
        for section, pieces in zip(X1_SECTION, X1_WORD_PIECES):
            load_scale_rows(section, 0)
            for first, end in pieces:
                load_words(section * PASSES + first, end - first)
        load_x2_words(3)

        def words_of(g):
            first = (g % RUN) * WORDS_OF_PASS
            return x2_runs[g // RUN][:].bitcast(F32)[:, :, first : first + WORDS_OF_PASS]

        def word_planes(g):
            words = words_of(g)
            return lambda t, u: words[:, t, u:WORDS_OF_PASS:2]

        def sort_x2(g):
            ordered = stage.tile([P, ROW_TILES, 2, P], F32, name="ordered")
            copy = nc.vector.tensor_copy if g in SORTED_BY_VECTOR else nc.scalar.copy
            copy(out=ordered[:], in_=words_of(g).rearrange("p t (w u) -> p t u w", u=2))
            return lambda t, u: ordered[:, t, u, :]

        def transpose_scene(planes, scene):
            xt = work.tile([P, 2, PAIRS_OF_SCENE], F32, tag="work", name="xt")
            for u in range(2):
                for half in range(2):
                    nc.tensor.transpose(
                        xt[:, u, half * P : (half + 1) * P],
                        planes(2 * scene + half, u),
                        ident[:],
                    )
            return xt

        def transpose_x2(planes):
            return [transpose_scene(planes, scene) for scene in range(SCENES)]

        def new_grouped():
            grouped = stage.tile([P, PAIRS, 4], BF16, align_bytes=64, name="grouped")
            return grouped

        def regroup_scene(grouped, scene, bank, copy):
            cols = slice(scene * PAIRS_OF_SCENE, (scene + 1) * PAIRS_OF_SCENE)
            copy(out=grouped[:].bitcast(F32)[:, cols, :], in_=bank[:].rearrange("p u r -> p r u"))

        def quantise_x2(g, grouped, first_scene, scenes):
            cols = slice(first_scene * PAIRS_OF_SCENE, (first_scene + scenes) * PAIRS_OF_SCENE)
            nc.vector.quantize_mx(
                out=x2_codes[:, AS_LIES, g, cols].bitcast(FP8X4),
                scales=x2_scales[:, AS_LIES, g, cols],
                in_=grouped[:, cols, :].rearrange("p r t -> p (r t)"),
            )

        def swap_x2(g, first_scene, scenes):
            cols = slice(first_scene * PAIRS_OF_SCENE, (first_scene + scenes) * PAIRS_OF_SCENE)
            for plane in (x2_codes[:].bitcast(I32), x2_scales[:]):
                nc.vector.tensor_copy(
                    out=plane[:, SWAPPED, g, cols].rearrange("p (b q r j) -> p b q j r", b=scenes, q=4, r=4),
                    in_=plane[:, AS_LIES, g, cols].rearrange("p (b j q r) -> p b q j r", b=scenes, q=4, r=4),
                )

        def prepare_x2(g, banks):
            grouped = new_grouped()
            for scene in range(SCENES):
                copy = nc.vector.tensor_copy if (g == RUN and scene == 1) else nc.scalar.copy
                regroup_scene(grouped, scene, banks[scene], copy)
            quantise_x2(g, grouped, 0, SCENES)
            swap_x2(g, 0, SCENES)

        def weight(section, g, first=0, width=OUT):
            w_pass = section * PASSES + g
            run_start = max(start for start, end in scale_runs[section] if start <= g)
            return dict(
                rhs=w_words[:, w_pass, 2 * first : 2 * (first + width)].bitcast(FP4X4),
                rhs_scale=w_scales[section, run_start][:, g - run_start, first : first + width],
            )

        def multiply_x2(t, g, orders=(AS_LIES, SWAPPED)):
            cols = slice(t * P, (t + 1) * P)
            for order in orders:
                nc.tensor.matmul_mx(
                    out=y_acc[t][:],
                    lhsT=x2_codes[:, order, g, cols].bitcast(FP8X4),
                    lhsT_scale=x2_scales[:, order, g, cols],
                    start=(g == 0 and order == AS_LIES),
                    stop=(g == PASSES - 1 and order == SWAPPED),
                    **weight(X2_SECTION[order], g),
                )

        def spread_bias():
            bias_all = work.tile([P, OUT], F32, tag="work", name="bias_all")
            nc.tensor.matmul(bias_all[:], lhsT=half_tile[:], rhs=bias_row[:], start=True, stop=True)
            return bias_all

        def transpose_x1():
            banks = []
            for local in range(2):
                first_word = local * WORDS_OF_PASS
                x1t = work.tile([P, 2, P], F32, tag="work", name="x1t")
                for u in range(2):
                    nc.tensor.transpose(
                        x1t[:, u, :],
                        x1_words[:, first_word + u : first_word + WORDS_OF_PASS : 2],
                        ident[:],
                    )
                banks.append(x1t)
            return banks

        def regroup_x1(banks):
            by_part = x1_grouped[:].bitcast(F32).rearrange("p (c l) h (k n) u -> p l h k c n u", l=2, k=2)
            for copy_of_x1 in range(2):
                for local, copy in enumerate((nc.scalar.copy, nc.vector.tensor_copy)):
                    copy(
                        out=by_part[:, local, 1, copy_of_x1],
                        in_=banks[local][:].rearrange("p u (r c) -> p c r u", c=X1_PARTS),
                    )
            for half in range(2):
                passes = slice(half * PASSES // 2, (half + 1) * PASSES // 2)
                cols = slice(passes.start * P, passes.stop * P)
                nc.vector.quantize_mx(
                    out=x1_codes[:, cols].bitcast(FP8X4),
                    scales=x1_scales[:, cols],
                    in_=x1_grouped[:, passes].rearrange("p g h n t -> p (g h n t)"),
                )
            nc.vector.tensor_reduce(
                out=low_rows[:],
                in_=ident[:].rearrange("p (h q r) -> p h q r", h=2, q=2)[:, :, 1, :],
                axis=AXES_XY,
                op=ADD,
            )

        def multiply_x1():
            ac = work.tile([P, OUT], F32, tag="work", name="ac")
            for section, first in ((X1_SECTION[0], HALF), (X1_SECTION[1], 0)):
                for g in range(PASSES):
                    cols = slice(g * P + first, (g + 1) * P + first)
                    nc.tensor.matmul_mx(
                        out=ac[:],
                        lhsT=x1_codes[:, cols].bitcast(FP8X4),
                        lhsT_scale=x1_scales[:, cols],
                        start=(section == X1_SECTION[0] and g == 0),
                        stop=(section == X1_SECTION[1] and g == PASSES - 1),
                        **weight(section, g),
                    )
            return ac

        def split_terms(ac):
            halves = [slice(half * OUT // 2, (half + 1) * OUT // 2) for half in range(2)]
            for cols in halves:
                nc.vector.tensor_tensor(out=terms[:, cols], in0=ac[:, cols], in1=bias_half[:, cols], op=ADD)
            for cols in halves:
                nc.vector.tensor_copy(out=terms_high[:, cols], in_=terms[:, cols])
            for cols in halves:
                nc.vector.scalar_tensor_tensor(
                    out=terms_split[:, cols],
                    in0=terms_high[:, cols],
                    scalar=low_rows[:],
                    in1=terms[:, cols],
                    op0=MULT,
                    op1=SUBTRACT,
                )

        def spread_terms(t):
            bank = work.tile([P, OUT], F32, tag="work", name="spread")
            nc.tensor.matmul(bank[:], lhsT=hot[:, t * P : (t + 1) * P], rhs=terms_split[:], start=True, stop=True)
            return bank

        out_by_tile = out.rearrange("b i j o -> (b i j) o").rearrange("(t p) o -> t p o", p=P)

        def copy_out(bank, copy):
            copied = stage.tile([P, OUT], F32, bufs=ROW_TILES, name="copied")
            copy(out=copied[:], in_=bank[:])
            return copied

        def finish(t, minuend, subtrahend, sign):
            parts = 2 if t == LAST_TILE else 1
            for part in range(parts):
                cols = slice(part * OUT // parts, (part + 1) * OUT // parts)
                joined = stage.tile([P, OUT // parts], F32, bufs=ROW_TILES + 1, name="joined")
                nc.vector.tensor_tensor(out=joined[:], in0=minuend[:, cols], in1=subtrahend[:, cols], op=SUBTRACT)
                result = stage.tile([P, OUT // parts], F32, bufs=ROW_TILES + 1, name="result")
                nc.scalar.activation(out=result[:], in_=joined[:], func=SIGMOID, scale=sign)
                nc.sync.dma_start(out=out_by_tile[t][:, cols], in_=result[:])

        def multiply_order(g, order):
            for t in range(ROW_TILES):
                multiply_x2(t, g, (order,))

        def multiply_all(g):
            multiply_order(g, AS_LIES)
            multiply_order(g, SWAPPED)

        def multiply_last(t, orders):
            for order in orders:
                for g in range(PASSES - RUN, PASSES):
                    multiply_x2(t, g, (order,))

        def warm_up(count):
            for n in range(count):
                nc.tensor.matmul(idle[:], lhsT=half_tile[:], rhs=zero_row[:], start=True, stop=True)

        idle = y_acc[LAST_TILE]
        warm_up(WARM_BEFORE)
        grouped = [new_grouped() for g in range(RUN)]
        for scene in range(SCENES):
            banks = [transpose_scene(word_planes(g), scene) for g in range(RUN)]
            if scene == 0:
                bias_all = spread_bias()
            warm_up(WARM_BETWEEN if scene == 0 else WARM_AFTER)
            for g in range(RUN):
                regroup_scene(grouped[g], scene, banks[g], nc.scalar.copy)
            quantise_x2(0, grouped[0], scene, 1)
            swap_x2(0, scene, 1)
        nc.scalar.copy(out=bias_half[:], in_=bias_all[:])
        quantise_x2(1, grouped[1], 0, SCENES)
        swap_x2(1, 0, SCENES)
        planes = {g: sort_x2(g) for g in range(RUN, 2 * RUN)}
        for scene in range(SCENES):
            for order in (AS_LIES, SWAPPED):
                for t in range(2 * scene, 2 * scene + 2):
                    multiply_x2(t, 0, (order,))
        multiply_order(1, AS_LIES)
        for g in range(RUN, PASSES):
            banks = transpose_x2(planes[g])
            if g == X1_WITH_PASS:
                regroup_x1(transpose_x1())
            prepare_x2(g, banks)
            if g + RUN < PASSES:
                planes[g + RUN] = sort_x2(g + RUN)
            if g == RUN:
                multiply_order(1, SWAPPED)
            elif g < PASSES - 1:
                multiply_all(g - 1)
        split_terms(multiply_x1())
        sums_of_tiles = []
        for t in (0, 1):
            multiply_last(t, (AS_LIES,))
        for t in (0, 1):
            multiply_last(t, (SWAPPED,))
            sums_of_tiles.append(copy_out(y_acc[t], nc.scalar.copy))
        banks = [spread_terms(t) for t in range(ROW_TILES)]
        spreads = {2: copy_out(banks[2], nc.scalar.copy)}
        for t in (0, 1):
            finish(t, banks[t], sums_of_tiles[t], -1.0)
        spreads[3] = copy_out(banks[3], nc.vector.tensor_copy)
        for t in (2, 3):
            multiply_last(t, (AS_LIES, SWAPPED))
            finish(t, y_acc[t], spreads[t], 1.0)
